import numpy as np
import ml_dtypes


def mxq(x, axis, fmt="e4m3"):
    dtype, down = {"e4m3": (ml_dtypes.float8_e4m3fn, 7), "e5m2": (ml_dtypes.float8_e5m2, 14)}[fmt]
    v = np.moveaxis(np.asarray(x, np.float32).astype(ml_dtypes.bfloat16).astype(np.float64), axis, -1)
    blocks = v.reshape(v.shape[:-1] + (-1, 32))
    amax = np.abs(blocks).max(-1, keepdims=True)
    byte = np.maximum(np.where(amax > 0, np.frexp(amax)[1] - 1 + 127, 0) - down, 1)
    scale = np.exp2(byte - 127.0)
    codes = (blocks / scale).astype(np.float32).astype(dtype).astype(np.float64)
    return np.moveaxis((codes * scale).reshape(v.shape), -1, axis)


WIDE = False


def mx_kscale(k):
    if not WIDE:
        return np.ones(k)
    levels = np.array([10, -10, 5, -5, 0])
    a = np.random.permutation(np.resize(levels, k // 512 * 4)).reshape(k // 512, 4)
    idx = np.arange(k)
    return np.exp2(a[idx // 512, idx % 128 // 32])


BF16 = ml_dtypes.bfloat16


def bf(x):
    return np.asarray(x, np.float32).astype(BF16)


def f64(x):
    return np.asarray(x).astype(np.float64)


B, T, C, H, D = 4, 1024, 256, 2, 256
HD = H * D


def unit_rms(u):
    return u / np.sqrt(np.mean(u * u, axis=-1, keepdims=True))


def setup_inputs():
    t = mx_kscale(HD)
    tv = t.reshape(H, D)
    a = (np.log(T) + 3.0) / np.sqrt(D)
    k = unit_rms(np.random.standard_normal((B, T, H, D)))
    idx = np.argsort(np.random.random((B, T, H)), axis=1)
    k_near = np.take_along_axis(k, idx[..., None], axis=1)
    q = unit_rms(a * k_near + np.sqrt(1.0 - a * a) * np.random.standard_normal((B, T, H, D)))
    return {
        "q_rot": bf(q),
        "k_rot": bf(k),
        "v": bf(np.random.standard_normal((B, T, H, D)) * 1.5 * tv),
        "v1": bf(np.random.standard_normal((B, T, H, D)) * 1.5 * tv),
        "lamb1": bf(0.5 + 0.1 * np.random.standard_normal(1)),
        "lamb2": bf(0.5 + 0.1 * np.random.standard_normal(1)),
        "wproj": bf(np.random.standard_normal((C, HD)) * 1.5 / np.sqrt(HD) / t[None, :]),
    }


def reference(q_rot, k_rot, v, v1, lamb1, lamb2, wproj):
    vm = f64(lamb1) * f64(v) + f64(lamb2) * f64(v1)
    s = f64(q_rot).transpose(0, 2, 1, 3) @ f64(k_rot).transpose(0, 2, 3, 1) * (1.0 / np.sqrt(D))
    e = np.exp(s - s.max(-1, keepdims=True))
    y = (mxq(e, 3, "e4m3") @ mxq(vm.transpose(0, 2, 1, 3), 2, "e4m3")) / e.sum(-1, keepdims=True)
    y = y.transpose(0, 2, 1, 3).reshape(B, T, HD)
    return mxq(y, 2, "e4m3") @ mxq(f64(wproj), 1, "e4m3").T

@@ -1,0 +1,346 @@
+from contextlib import ExitStack
+
+import concourse.mybir as mybir
+from concourse.masks import make_identity
+
+F32 = mybir.dt.float32
+BF16 = mybir.dt.bfloat16
+U32 = mybir.dt.uint32
+U8 = mybir.dt.uint8
+FP8X4 = mybir.dt.float8_e4m3fn_x4
+ALU = mybir.AluOpType
+ACT = mybir.ActivationFunctionType
+
+B, T, H, D = 4, 1024, 2, 256
+HD = H * D
+C = 256
+P = 128
+PACK = 4
+K_PASS = P * PACK
+PASSES = T // K_PASS
+TILES = T // P
+BANK = 512
+HALVES = T // BANK
+WORDS = D // 2
+SCALE = 1.0 / 16.0
+
+HEADS = B * H
+STEPS = HEADS * TILES
+PAIRS = STEPS // 2
+OUT_PAIRS = B * TILES // 2
+FLIP_LAG = 3
+QUANT_LAG = 4
+PV_LAG = 8
+Y_LAG = PV_LAG + TILES + 3
+OUT_LAG = Y_LAG + 2
+W_ROUND = 2
+ROUNDS = 4 * (OUT_PAIRS - 1) + OUT_LAG + 1
+
+FLOPS = 2 * B * H * T * T * D * 2 + 2 * B * T * HD * C
+
+
+def tile_selfattention_pb_t_kernel(tc, q_rot, k_rot, v, v1, lamb1, lamb2, wproj, out):
+    nc = tc.nc
+    with ExitStack() as ctx:
+        const = ctx.enter_context(tc.tile_pool(name="const", bufs=1))
+        loads = ctx.enter_context(tc.tile_pool(name="loads", bufs=2))
+        heads = ctx.enter_context(tc.tile_pool(name="heads", bufs=2))
+        steps = ctx.enter_context(tc.tile_pool(name="steps", bufs=3))
+        mixing = ctx.enter_context(tc.tile_pool(name="mixing", bufs=1))
+        psum_scores = ctx.enter_context(tc.psum_pool(name="psum_scores", bufs=2 * HALVES))
+        psum_flips = ctx.enter_context(tc.psum_pool(name="psum_flips", bufs=2))
+        psum_other = ctx.enter_context(tc.psum_pool(name="psum_other", bufs=2))
+        ctx.enter_context(tc.manual_schedule())
+
+        ident_bf = const.tile([P, P], BF16)
+        make_identity(nc, ident_bf[:])
+        ident_f32 = const.tile([P, P], F32)
+        make_identity(nc, ident_f32[:])
+
+        raw = {}
+
+        def load_tokens(name, source, b):
+            tokens = loads.tile([P, TILES, HD], BF16, name=name)
+            for g in range(PASSES):
+                nc.sync.dma_start(
+                    out=tokens[:, g * PACK : (g + 1) * PACK, :].rearrange("p t f -> p (t f)"),
+                    in_=source[b, g * K_PASS : (g + 1) * K_PASS].rearrange("(p t) h d -> p (t h d)", p=P),
+                )
+            raw[(name, b)] = tokens
+
+        def load_batch(b):
+            load_tokens("k_raw", k_rot, b)
+            load_tokens("q_raw", q_rot, b)
+            load_tokens("v_raw", v, b)
+            load_tokens("v1_raw", v1, b)
+
+        load_batch(0)
+        w_raw = const.tile([P, C // P, HD], BF16)
+        nc.sync.dma_start(out=w_raw[:], in_=wproj.rearrange("(o p) k -> p o k", p=P))
+        lam1_bf = const.tile([P, 1], BF16)
+        nc.gpsimd.dma_start(out=lam1_bf[:], in_=lamb1.partition_broadcast(P))
+        lam2_bf = const.tile([P, 1], BF16)
+        nc.gpsimd.dma_start(out=lam2_bf[:], in_=lamb2.partition_broadcast(P))
+        lam1 = const.tile([P, 1], F32)
+        nc.gpsimd.tensor_copy(out=lam1[:], in_=lam1_bf[:])
+        lam2 = const.tile([P, 1], F32)
+        nc.gpsimd.tensor_copy(out=lam2[:], in_=lam2_bf[:])
+
+        vm_grouped = {}
+        vm_codes = {}
+        vm_scales = {}
+
+        def mix_values(head):
+            b, h = divmod(head, H)
+            features = slice(h * D, (h + 1) * D)
+            grouped = heads.tile([P, PASSES, D, PACK], BF16, name="vm_grouped", align_bytes=64)
+            for g in range(PASSES):
+                tiles_of_pass = slice(g * PACK, (g + 1) * PACK)
+                part1 = mixing.tile([P, PACK, D], F32, name="part1")
+                nc.gpsimd.tensor_scalar(
+                    out=part1[:], in0=raw[("v_raw", b)][:, tiles_of_pass, features],
+                    scalar1=lam1[:, 0:1], scalar2=0.0, op0=ALU.mult, op1=ALU.add,
+                )
+                part2 = mixing.tile([P, PACK, D], F32, name="part2")
+                nc.gpsimd.tensor_scalar(
+                    out=part2[:], in0=raw[("v1_raw", b)][:, tiles_of_pass, features],
+                    scalar1=lam2[:, 0:1], scalar2=0.0, op0=ALU.mult, op1=ALU.add,
+                )
+                nc.gpsimd.tensor_tensor(
+                    out=grouped[:, g, :, :],
+                    in0=part1[:].rearrange("p t d -> p d t"),
+                    in1=part2[:].rearrange("p t d -> p d t"),
+                    op=ALU.add,
+                )
+            vm_grouped[head] = grouped
+
+        def quantise_values(head):
+            codes = heads.tile([P, PASSES, D], U32, name="vm_codes", align_bytes=64)
+            scales = heads.tile([P, PASSES, D], U8, name="vm_scales", align_bytes=64)
+            nc.vector.quantize_mx(
+                out=codes[:].rearrange("p g d -> p (g d)").bitcast(FP8X4),
+                scales=scales[:].rearrange("p g d -> p (g d)"),
+                in_=vm_grouped[head][:].rearrange("p g d t -> p (g d t)"),
+            )
+            vm_codes[head] = codes
+            vm_scales[head] = scales
+
+        mix_values(0)
+
+        w_codes = const.tile([P, C], U32, align_bytes=64)
+        w_scales = const.tile([P, C], U8, align_bytes=64)
+
+        def prepare_weights():
+            w_flipped = psum_other.tile([P, PACK, C], BF16, name="other_bank")
+            for o in range(C // P):
+                for t in range(PACK):
+                    nc.tensor.transpose(
+                        w_flipped[:, t, o * P : (o + 1) * P], w_raw[:, o, t * P : (t + 1) * P], ident_bf[:]
+                    )
+            w_grouped = const.tile([P, C, PACK], BF16, align_bytes=64)
+            nc.vector.tensor_copy(out=w_grouped[:], in_=w_flipped[:].rearrange("p t c -> p c t"))
+            nc.vector.quantize_mx(
+                out=w_codes[:].bitcast(FP8X4), scales=w_scales[:],
+                in_=w_grouped[:].rearrange("p c t -> p (c t)"),
+            )
+
+        flipped_words = {}
+        flipped_heads = {}
+
+        def flip_half_head(name, head, half):
+            b, h = divmod(head, H)
+            words = (
+                raw[(name + "_raw", b)][:]
+                .rearrange("p c f -> p (c f)")
+                .bitcast(F32)
+                .rearrange("p (c w) -> p c w", c=TILES)
+            )
+            if half == 0:
+                flipped = heads.tile([P, T], F32, name=name + "_flipped")
+                flipped_words[(name, head)] = flipped
+                flipped_heads[(name, head)] = flipped[:].bitcast(BF16).rearrange("p (n e) -> p n e", e=2)
+            bank = psum_other.tile([P, PACK, P], F32, name="other_bank")
+            for j in range(PACK):
+                nc.tensor.transpose(
+                    bank[:, j, :], words[:, half * PACK + j, h * WORDS : (h + 1) * WORDS], ident_f32[:]
+                )
+            nc.vector.tensor_copy(
+                out=flipped_words[(name, head)][:, half * BANK : (half + 1) * BANK],
+                in_=bank[:].rearrange("p j r -> p (j r)"),
+            )
+
+        for name in ("k", "q"):
+            for half in range(HALVES):
+                flip_half_head(name, 0, half)
+
+        score_banks = {}
+        negated_scores = {}
+        biases = {}
+        row_sums = {}
+        probs = {}
+        probs_grouped = {}
+        e_codes = {}
+        e_scales = {}
+
+        def score_matmul(step, half, parity):
+            head, tile_index = divmod(step, TILES)
+            if parity == 0:
+                score_banks[(step, half)] = psum_scores.tile([P, BANK], F32, name="score_bank")
+            nc.tensor.matmul(
+                score_banks[(step, half)][:],
+                lhsT=flipped_heads[("q", head)][:, tile_index * P : (tile_index + 1) * P, parity],
+                rhs=flipped_heads[("k", head)][:, half * BANK : (half + 1) * BANK, parity],
+                start=(parity == 0),
+                stop=(parity == 1),
+            )
+
+        def scale_and_bound(step):
+            negated = steps.tile([P, T], F32, name="negated")
+            first_min = steps.tile([P, 1], F32, name="first_min")
+            bias = steps.tile([P, 1], F32, name="bias")
+            nc.vector.tensor_scalar(
+                out=negated[:, 0:BANK], in0=score_banks[(step, 0)][:], scalar1=-SCALE, scalar2=None,
+                op0=ALU.mult, op1=ALU.min, accum_out=first_min[:],
+            )
+            nc.vector.tensor_scalar(
+                out=negated[:, BANK:T], in0=score_banks[(step, 1)][:], scalar1=-SCALE, scalar2=first_min[:, 0:1],
+                op0=ALU.mult, op1=ALU.min, accum_out=bias[:],
+            )
+            negated_scores[step] = negated
+            biases[step] = bias
+
+        def exponentials(step):
+            head, tile_index = divmod(step, TILES)
+            if tile_index == 0:
+                row_sums[head] = heads.tile([P, TILES], F32, name="row_sums")
+            e_rows = steps.tile([P, T], BF16, name="e_rows", bufs=FLIP_LAG + 2)
+            nc.scalar.activation(
+                out=e_rows[:], in_=negated_scores[step][:], func=ACT.Exp, bias=biases[step][:, 0:1], scale=-1.0,
+                accum_out=row_sums[head][:, tile_index : tile_index + 1],
+            )
+            probs[step] = e_rows
+
+        def group_probabilities(step, e_flipped):
+            grouped = steps.tile([P, PASSES, P, PACK], BF16, name="e_grouped", align_bytes=64)
+            nc.scalar.copy(out=grouped[:], in_=e_flipped[:].rearrange("p (g t) q -> p g q t", g=PASSES))
+            probs_grouped[step] = grouped
+
+        def quantise_probabilities(step):
+            head, tile_index = divmod(step, TILES)
+            if tile_index == 0:
+                e_codes[head] = heads.tile([P, TILES, PASSES, P], U32, name="e_codes", align_bytes=64)
+                e_scales[head] = heads.tile([P, TILES, PASSES, P], U8, name="e_scales", align_bytes=64)
+            nc.vector.quantize_mx(
+                out=e_codes[head][:, tile_index, :, :].rearrange("p g q -> p (g q)").bitcast(FP8X4),
+                scales=e_scales[head][:, tile_index, :, :].rearrange("p g q -> p (g q)"),
+                in_=probs_grouped[step][:].rearrange("p g q t -> p (g q t)"),
+            )
+
+        y_rows = {}
+        y_codes = {}
+        y_scales = {}
+
+        def attend(pair):
+            head, pair_in_head = divmod(pair, TILES // 2)
+            b, h = divmod(head, H)
+            first = 2 * pair_in_head
+            if h == 0 and pair_in_head == 0:
+                y_rows[b] = heads.tile([P, TILES, HD], BF16, name="y_rows")
+            inverse = steps.tile([P, 2], F32, name="inverse")
+            nc.vector.reciprocal(out=inverse[:], in_=row_sums[head][:, first : first + 2])
+            bank = psum_other.tile([P, 2, D], F32, name="other_bank")
+            for i in range(2):
+                for g in range(PASSES):
+                    nc.tensor.matmul_mx(
+                        out=bank[:, i, :],
+                        lhsT=e_codes[head][:, first + i, g, :].bitcast(FP8X4),
+                        lhsT_scale=e_scales[head][:, first + i, g, :],
+                        rhs=vm_codes[head][:, g, :].bitcast(FP8X4),
+                        rhs_scale=vm_scales[head][:, g, :],
+                        start=(g == 0),
+                        stop=(g == PASSES - 1),
+                    )
+            for i in range(2):
+                nc.vector.tensor_scalar(
+                    out=y_rows[b][:, first + i, h * D : (h + 1) * D], in0=bank[:, i, :],
+                    scalar1=inverse[:, i : i + 1], scalar2=None, op0=ALU.mult,
+                )
+
+        def flip_outputs(out_pair):
+            b, pair_in_batch = divmod(out_pair, TILES // 2)
+            first = 2 * pair_in_batch
+            bank = psum_other.tile([P, 2, PACK, P], BF16, name="other_bank")
+            for i in range(2):
+                for t in range(PACK):
+                    nc.tensor.transpose(bank[:, i, t, :], y_rows[b][:, first + i, t * P : (t + 1) * P], ident_bf[:])
+            grouped = steps.tile([P, 2, P, PACK], BF16, name="y_grouped", align_bytes=64)
+            nc.vector.tensor_copy(out=grouped[:], in_=bank[:].rearrange("p i t q -> p i q t"))
+            codes = steps.tile([P, 2, P], U32, name="y_codes", align_bytes=64)
+            scales = steps.tile([P, 2, P], U8, name="y_scales", align_bytes=64)
+            nc.vector.quantize_mx(
+                out=codes[:].rearrange("p i q -> p (i q)").bitcast(FP8X4),
+                scales=scales[:].rearrange("p i q -> p (i q)"),
+                in_=grouped[:].rearrange("p i q t -> p (i q t)"),
+            )
+            y_codes[out_pair] = codes
+            y_scales[out_pair] = scales
+
+        def project(out_pair):
+            b, pair_in_batch = divmod(out_pair, TILES // 2)
+            g, t_first = divmod(2 * pair_in_batch, PACK)
+            bank = psum_other.tile([P, 2, C], F32, name="other_bank")
+            for i in range(2):
+                nc.tensor.matmul_mx(
+                    out=bank[:, i, :],
+                    lhsT=y_codes[out_pair][:, i, :].bitcast(FP8X4),
+                    lhsT_scale=y_scales[out_pair][:, i, :],
+                    rhs=w_codes[:].bitcast(FP8X4),
+                    rhs_scale=w_scales[:],
+                    start=True,
+                    stop=True,
+                )
+            result = steps.tile([P, 2, C], F32, name="result")
+            nc.scalar.copy(out=result[:], in_=bank[:])
+            tokens_of_pass = out[b, g * K_PASS : (g + 1) * K_PASS, :].rearrange("(p t) c -> p t c", t=PACK)
+            nc.sync.dma_start(out=tokens_of_pass[:, t_first : t_first + 2, :], in_=result[:])
+
+        for r in range(ROUNDS):
+            next_batch = r // (H * TILES) + 1
+            if r % (H * TILES) == 0 and next_batch < B:
+                load_batch(next_batch)
+            next_head = r // TILES + 1
+            if r % TILES == 0 and next_head < HEADS:
+                mix_values(next_head)
+
+            flipping = 0 <= r - FLIP_LAG < STEPS
+            if flipping:
+                e_flipped = psum_flips.tile([P, TILES, P], BF16, name="e_flipped")
+            for piece in range(2 * HALVES):
+                if r < STEPS:
+                    score_matmul(r, piece // 2, piece % 2)
+                if flipping:
+                    for c in (2 * piece, 2 * piece + 1):
+                        nc.tensor.transpose(
+                            e_flipped[:, c, :], probs[r - FLIP_LAG][:, c * P : (c + 1) * P], ident_bf[:]
+                        )
+            if r < STEPS:
+                scale_and_bound(r)
+            if flipping:
+                group_probabilities(r - FLIP_LAG, e_flipped)
+            if r < STEPS:
+                exponentials(r)
+            if 0 <= r - QUANT_LAG < STEPS:
+                quantise_probabilities(r - QUANT_LAG)
+
+            if r % 4 < HALVES and next_head < HEADS:
+                flip_half_head("k" if r % TILES < 4 else "q", next_head, r % 4)
+            if r == W_ROUND:
+                prepare_weights()
+            if (r + 1 - PV_LAG) % TILES == 0 and 0 <= (r + 1 - PV_LAG) // TILES < HEADS:
+                quantise_values((r + 1 - PV_LAG) // TILES)
+            if (r - PV_LAG) % 2 == 0 and 0 <= (r - PV_LAG) // 2 < PAIRS:
+                attend((r - PV_LAG) // 2)
+            if (r - Y_LAG) % 4 == 0 and 0 <= (r - Y_LAG) // 4 < OUT_PAIRS:
+                flip_outputs((r - Y_LAG) // 4)
+            if (r - OUT_LAG) % 4 == 0 and 0 <= (r - OUT_LAG) // 4 < OUT_PAIRS:
+                project((r - OUT_LAG) // 4)

@@ -46,7 +46,7 @@ def tile_selfattention_pb_t_kernel(tc, q_rot, k_rot, v, v1, lamb1, lamb2, wproj,
         loads = ctx.enter_context(tc.tile_pool(name="loads", bufs=2))
         heads = ctx.enter_context(tc.tile_pool(name="heads", bufs=2))
         steps = ctx.enter_context(tc.tile_pool(name="steps", bufs=3))
-        mixing = ctx.enter_context(tc.tile_pool(name="mixing", bufs=1))
+        mixing = ctx.enter_context(tc.tile_pool(name="mixing", bufs=2))
         psum_scores = ctx.enter_context(tc.psum_pool(name="psum_scores", bufs=2 * HALVES))
         psum_flips = ctx.enter_context(tc.psum_pool(name="psum_flips", bufs=2))
         psum_other = ctx.enter_context(tc.psum_pool(name="psum_other", bufs=2))
@@ -82,37 +82,32 @@ def tile_selfattention_pb_t_kernel(tc, q_rot, k_rot, v, v1, lamb1, lamb2, wproj,
         lam2_bf = const.tile([P, 1], BF16)
         nc.gpsimd.dma_start(out=lam2_bf[:], in_=lamb2.partition_broadcast(P))
         lam1 = const.tile([P, 1], F32)
-        nc.gpsimd.tensor_copy(out=lam1[:], in_=lam1_bf[:])
+        nc.vector.tensor_copy(out=lam1[:], in_=lam1_bf[:])
         lam2 = const.tile([P, 1], F32)
-        nc.gpsimd.tensor_copy(out=lam2[:], in_=lam2_bf[:])
+        nc.vector.tensor_copy(out=lam2[:], in_=lam2_bf[:])
 
         vm_grouped = {}
         vm_codes = {}
         vm_scales = {}
 
-        def mix_values(head):
+        def mix_values(head, g):
             b, h = divmod(head, H)
             features = slice(h * D, (h + 1) * D)
-            grouped = heads.tile([P, PASSES, D, PACK], BF16, name="vm_grouped", align_bytes=64)
-            for g in range(PASSES):
-                tiles_of_pass = slice(g * PACK, (g + 1) * PACK)
-                part1 = mixing.tile([P, PACK, D], F32, name="part1")
-                nc.gpsimd.tensor_scalar(
-                    out=part1[:], in0=raw[("v_raw", b)][:, tiles_of_pass, features],
-                    scalar1=lam1[:, 0:1], scalar2=0.0, op0=ALU.mult, op1=ALU.add,
-                )
-                part2 = mixing.tile([P, PACK, D], F32, name="part2")
-                nc.gpsimd.tensor_scalar(
-                    out=part2[:], in0=raw[("v1_raw", b)][:, tiles_of_pass, features],
-                    scalar1=lam2[:, 0:1], scalar2=0.0, op0=ALU.mult, op1=ALU.add,
-                )
-                nc.gpsimd.tensor_tensor(
-                    out=grouped[:, g, :, :],
-                    in0=part1[:].rearrange("p t d -> p d t"),
-                    in1=part2[:].rearrange("p t d -> p d t"),
-                    op=ALU.add,
-                )
-            vm_grouped[head] = grouped
+            tiles_of_pass = slice(g * PACK, (g + 1) * PACK)
+            if g == 0:
+                vm_grouped[head] = heads.tile([P, PASSES, D, PACK], BF16, name="vm_grouped", align_bytes=64)
+            part2 = mixing.tile([P, PACK, D], F32, name="part2")
+            nc.scalar.activation(
+                out=part2[:], in_=raw[("v1_raw", b)][:, tiles_of_pass, features], func=ACT.Copy, scale=lam2[:, 0:1]
+            )
+            nc.vector.scalar_tensor_tensor(
+                out=vm_grouped[head][:, g, :, :],
+                in0=raw[("v_raw", b)][:, tiles_of_pass, features].rearrange("p t d -> p d t"),
+                scalar=lam1[:, 0:1],
+                in1=part2[:].rearrange("p t d -> p d t"),
+                op0=ALU.mult,
+                op1=ALU.add,
+            )
 
         def quantise_values(head):
             codes = heads.tile([P, PASSES, D], U32, name="vm_codes", align_bytes=64)
@@ -124,8 +119,6 @@ def tile_selfattention_pb_t_kernel(tc, q_rot, k_rot, v, v1, lamb1, lamb2, wproj,
             )
             vm_codes[head] = codes
             vm_scales[head] = scales
-
-        mix_values(0)
 
         w_codes = const.tile([P, C], U32, align_bytes=64)
         w_scales = const.tile([P, C], U8, align_bytes=64)
@@ -309,8 +302,6 @@ def tile_selfattention_pb_t_kernel(tc, q_rot, k_rot, v, v1, lamb1, lamb2, wproj,
             if r % (H * TILES) == 0 and next_batch < B:
                 load_batch(next_batch)
             next_head = r // TILES + 1
-            if r % TILES == 0 and next_head < HEADS:
-                mix_values(next_head)
 
             flipping = 0 <= r - FLIP_LAG < STEPS
             if flipping:
@@ -336,6 +327,8 @@ def tile_selfattention_pb_t_kernel(tc, q_rot, k_rot, v, v1, lamb1, lamb2, wproj,
                 flip_half_head("k" if r % TILES < 4 else "q", next_head, r % 4)
             if r == W_ROUND:
                 prepare_weights()
+            if r % 4 == 2 and r < STEPS:
+                mix_values(r // TILES, (r % TILES) // 4)
             if (r + 1 - PV_LAG) % TILES == 0 and 0 <= (r + 1 - PV_LAG) // TILES < HEADS:
                 quantise_values((r + 1 - PV_LAG) // TILES)
             if (r - PV_LAG) % 2 == 0 and 0 <= (r - PV_LAG) // 2 < PAIRS:

@@ -24,17 +24,22 @@ HALVES = T // BANK
 WORDS = D // 2
 SCALE = 1.0 / 16.0
 
-HEADS = B * H
-STEPS = HEADS * TILES
+STEPS_PER_BATCH = H * TILES
+STEPS = B * STEPS_PER_BATCH
 PAIRS = STEPS // 2
-OUT_PAIRS = B * TILES // 2
+QUADS = STEPS // 4
 FLIP_LAG = 3
-QUANT_LAG = 4
-PV_LAG = 8
-Y_LAG = PV_LAG + TILES + 3
+QUANT_LAG = 5
+PV_LAG = 6
+Y_LAG = PV_LAG + 3
 OUT_LAG = Y_LAG + 2
-W_ROUND = 2
-ROUNDS = 4 * (OUT_PAIRS - 1) + OUT_LAG + 1
+W_ROUND = 1
+MIX_ROUND = 0
+ROUNDS = 4 * (QUADS - 1) + OUT_LAG + 2
+FLIP_ORDER = (
+    ("k", 0, 0), ("k", 0, 1), ("q", 0, 0), ("k", 1, 0), ("k", 1, 1), ("q", 1, 0), ("q", 0, 1), ("q", 1, 1),
+)
+FLIPS_AHEAD = 6
 
 FLOPS = 2 * B * H * T * T * D * 2 + 2 * B * T * HD * C
 
@@ -44,12 +49,11 @@ def tile_selfattention_pb_t_kernel(tc, q_rot, k_rot, v, v1, lamb1, lamb2, wproj,
     with ExitStack() as ctx:
         const = ctx.enter_context(tc.tile_pool(name="const", bufs=1))
         loads = ctx.enter_context(tc.tile_pool(name="loads", bufs=2))
-        heads = ctx.enter_context(tc.tile_pool(name="heads", bufs=2))
+        batches = ctx.enter_context(tc.tile_pool(name="batches", bufs=2))
         steps = ctx.enter_context(tc.tile_pool(name="steps", bufs=3))
-        mixing = ctx.enter_context(tc.tile_pool(name="mixing", bufs=2))
-        psum_scores = ctx.enter_context(tc.psum_pool(name="psum_scores", bufs=2 * HALVES))
+        psum_scores = ctx.enter_context(tc.psum_pool(name="psum_scores", bufs=3))
         psum_flips = ctx.enter_context(tc.psum_pool(name="psum_flips", bufs=2))
-        psum_other = ctx.enter_context(tc.psum_pool(name="psum_other", bufs=2))
+        psum_other = ctx.enter_context(tc.psum_pool(name="psum_other", bufs=3))
         ctx.enter_context(tc.manual_schedule())
 
         ident_bf = const.tile([P, P], BF16)
@@ -74,51 +78,52 @@ def tile_selfattention_pb_t_kernel(tc, q_rot, k_rot, v, v1, lamb1, lamb2, wproj,
             load_tokens("v_raw", v, b)
             load_tokens("v1_raw", v1, b)
 
+        lam1_bf = const.tile([P, 1], BF16)
+        nc.sync.dma_start(out=lam1_bf[:], in_=lamb1.partition_broadcast(P))
+        lam2_bf = const.tile([P, 1], BF16)
+        nc.sync.dma_start(out=lam2_bf[:], in_=lamb2.partition_broadcast(P))
         load_batch(0)
         w_raw = const.tile([P, C // P, HD], BF16)
         nc.sync.dma_start(out=w_raw[:], in_=wproj.rearrange("(o p) k -> p o k", p=P))
-        lam1_bf = const.tile([P, 1], BF16)
-        nc.gpsimd.dma_start(out=lam1_bf[:], in_=lamb1.partition_broadcast(P))
-        lam2_bf = const.tile([P, 1], BF16)
-        nc.gpsimd.dma_start(out=lam2_bf[:], in_=lamb2.partition_broadcast(P))
+        load_batch(1)
         lam1 = const.tile([P, 1], F32)
-        nc.vector.tensor_copy(out=lam1[:], in_=lam1_bf[:])
         lam2 = const.tile([P, 1], F32)
-        nc.vector.tensor_copy(out=lam2[:], in_=lam2_bf[:])
 
+        second_terms = {}
         vm_grouped = {}
         vm_codes = {}
         vm_scales = {}
 
-        def mix_values(head, g):
-            b, h = divmod(head, H)
-            features = slice(h * D, (h + 1) * D)
-            tiles_of_pass = slice(g * PACK, (g + 1) * PACK)
-            if g == 0:
-                vm_grouped[head] = heads.tile([P, PASSES, D, PACK], BF16, name="vm_grouped", align_bytes=64)
-            part2 = mixing.tile([P, PACK, D], F32, name="part2")
+        def scale_second_values(b, h, g):
+            term = steps.tile([P, PACK, D], F32, name="second_term")
             nc.scalar.activation(
-                out=part2[:], in_=raw[("v1_raw", b)][:, tiles_of_pass, features], func=ACT.Copy, scale=lam2[:, 0:1]
+                out=term[:], in_=raw[("v1_raw", b)][:, g * PACK : (g + 1) * PACK, h * D : (h + 1) * D],
+                func=ACT.Copy, scale=lam2[:, 0:1],
             )
+            second_terms[(b, h, g)] = term
+
+        def mix_values(b, h, g):
+            if g == 0:
+                vm_grouped[(b, h)] = steps.tile([P, PASSES, D, PACK], BF16, name="vm_grouped", align_bytes=64)
             nc.vector.scalar_tensor_tensor(
-                out=vm_grouped[head][:, g, :, :],
-                in0=raw[("v_raw", b)][:, tiles_of_pass, features].rearrange("p t d -> p d t"),
+                out=vm_grouped[(b, h)][:, g, :, :],
+                in0=raw[("v_raw", b)][:, g * PACK : (g + 1) * PACK, h * D : (h + 1) * D].rearrange("p t d -> p d t"),
                 scalar=lam1[:, 0:1],
-                in1=part2[:].rearrange("p t d -> p d t"),
+                in1=second_terms[(b, h, g)][:].rearrange("p t d -> p d t"),
                 op0=ALU.mult,
                 op1=ALU.add,
             )
 
-        def quantise_values(head):
-            codes = heads.tile([P, PASSES, D], U32, name="vm_codes", align_bytes=64)
-            scales = heads.tile([P, PASSES, D], U8, name="vm_scales", align_bytes=64)
+        def quantise_values(b, h):
+            codes = batches.tile([P, PASSES, D], U32, name="vm_codes%d" % h, align_bytes=64)
+            scales = batches.tile([P, PASSES, D], U8, name="vm_scales%d" % h, align_bytes=64)
             nc.vector.quantize_mx(
                 out=codes[:].rearrange("p g d -> p (g d)").bitcast(FP8X4),
                 scales=scales[:].rearrange("p g d -> p (g d)"),
-                in_=vm_grouped[head][:].rearrange("p g d t -> p (g d t)"),
+                in_=vm_grouped[(b, h)][:].rearrange("p g d t -> p (g d t)"),
             )
-            vm_codes[head] = codes
-            vm_scales[head] = scales
+            vm_codes[(b, h)] = codes
+            vm_scales[(b, h)] = scales
 
         w_codes = const.tile([P, C], U32, align_bytes=64)
         w_scales = const.tile([P, C], U8, align_bytes=64)
@@ -138,36 +143,45 @@ def tile_selfattention_pb_t_kernel(tc, q_rot, k_rot, v, v1, lamb1, lamb2, wproj,
             )
 
         flipped_words = {}
-        flipped_heads = {}
+        flipped_pairs = {}
 
-        def flip_half_head(name, head, half):
-            b, h = divmod(head, H)
+        other_banks = {}
+
+        def flip_half_head(unit):
+            b, k = divmod(unit, len(FLIP_ORDER))
+            name, h, half = FLIP_ORDER[k]
             words = (
                 raw[(name + "_raw", b)][:]
                 .rearrange("p c f -> p (c f)")
                 .bitcast(F32)
                 .rearrange("p (c w) -> p c w", c=TILES)
             )
-            if half == 0:
-                flipped = heads.tile([P, T], F32, name=name + "_flipped")
-                flipped_words[(name, head)] = flipped
-                flipped_heads[(name, head)] = flipped[:].bitcast(BF16).rearrange("p (n e) -> p n e", e=2)
+            if (name, b) not in flipped_words:
+                flipped = batches.tile([P, H, T], F32, name=name + "_flipped")
+                flipped_words[(name, b)] = flipped
+                flipped_pairs[(name, b)] = (
+                    flipped[:].rearrange("p h n -> p (h n)").bitcast(BF16).rearrange("p (h n e) -> p h n e", h=H, e=2)
+                )
             bank = psum_other.tile([P, PACK, P], F32, name="other_bank")
             for j in range(PACK):
                 nc.tensor.transpose(
                     bank[:, j, :], words[:, half * PACK + j, h * WORDS : (h + 1) * WORDS], ident_f32[:]
                 )
-            nc.vector.tensor_copy(
-                out=flipped_words[(name, head)][:, half * BANK : (half + 1) * BANK],
-                in_=bank[:].rearrange("p j r -> p (j r)"),
-            )
+            other_banks[("flip", unit)] = bank
 
-        for name in ("k", "q"):
-            for half in range(HALVES):
-                flip_half_head(name, 0, half)
+        def keep_half_head(unit):
+            b, k = divmod(unit, len(FLIP_ORDER))
+            name, h, half = FLIP_ORDER[k]
+            target = flipped_words[(name, b)][:, h, half * BANK : (half + 1) * BANK]
+            bank = other_banks[("flip", unit)]
+            if unit % 2 == 0:
+                nc.scalar.copy(out=target, in_=bank[:].rearrange("p j r -> p (j r)"))
+            else:
+                nc.vector.tensor_copy(out=target, in_=bank[:].rearrange("p j r -> p (j r)"))
 
         score_banks = {}
         negated_scores = {}
+        first_mins = {}
         biases = {}
         row_sums = {}
         probs = {}
@@ -175,41 +189,43 @@ def tile_selfattention_pb_t_kernel(tc, q_rot, k_rot, v, v1, lamb1, lamb2, wproj,
         e_codes = {}
         e_scales = {}
 
+        def place(step):
+            b, rest = divmod(step, STEPS_PER_BATCH)
+            j, rest = divmod(rest, 2 * H)
+            h, i = divmod(rest, 2)
+            return b, h, 2 * j + i
+
         def score_matmul(step, half, parity):
-            head, tile_index = divmod(step, TILES)
+            b, h, tile_index = place(step)
             if parity == 0:
                 score_banks[(step, half)] = psum_scores.tile([P, BANK], F32, name="score_bank")
             nc.tensor.matmul(
                 score_banks[(step, half)][:],
-                lhsT=flipped_heads[("q", head)][:, tile_index * P : (tile_index + 1) * P, parity],
-                rhs=flipped_heads[("k", head)][:, half * BANK : (half + 1) * BANK, parity],
+                lhsT=flipped_pairs[("q", b)][:, h, tile_index * P : (tile_index + 1) * P, parity],
+                rhs=flipped_pairs[("k", b)][:, h, half * BANK : (half + 1) * BANK, parity],
                 start=(parity == 0),
                 stop=(parity == 1),
             )
 
-        def scale_and_bound(step):
-            negated = steps.tile([P, T], F32, name="negated")
-            first_min = steps.tile([P, 1], F32, name="first_min")
-            bias = steps.tile([P, 1], F32, name="bias")
+        def scale_and_bound(step, half):
+            if half == 0:
+                negated_scores[step] = steps.tile([P, T], F32, name="negated")
+                first_mins[step] = steps.tile([P, 1], F32, name="first_min")
+                biases[step] = steps.tile([P, 1], F32, name="bias")
             nc.vector.tensor_scalar(
-                out=negated[:, 0:BANK], in0=score_banks[(step, 0)][:], scalar1=-SCALE, scalar2=None,
-                op0=ALU.mult, op1=ALU.min, accum_out=first_min[:],
+                out=negated_scores[step][:, half * BANK : (half + 1) * BANK], in0=score_banks[(step, half)][:],
+                scalar1=-SCALE, scalar2=(None if half == 0 else first_mins[step][:, 0:1]),
+                op0=ALU.mult, op1=ALU.min,
+                accum_out=(first_mins[step][:] if half == 0 else biases[step][:]),
             )
-            nc.vector.tensor_scalar(
-                out=negated[:, BANK:T], in0=score_banks[(step, 1)][:], scalar1=-SCALE, scalar2=first_min[:, 0:1],
-                op0=ALU.mult, op1=ALU.min, accum_out=bias[:],
-            )
-            negated_scores[step] = negated
-            biases[step] = bias
 
         def exponentials(step):
-            head, tile_index = divmod(step, TILES)
-            if tile_index == 0:
-                row_sums[head] = heads.tile([P, TILES], F32, name="row_sums")
+            if step % 2 == 0:
+                row_sums[step // 2] = steps.tile([P, 2], F32, name="row_sums", bufs=PV_LAG // 2 + 2)
             e_rows = steps.tile([P, T], BF16, name="e_rows", bufs=FLIP_LAG + 2)
             nc.scalar.activation(
                 out=e_rows[:], in_=negated_scores[step][:], func=ACT.Exp, bias=biases[step][:, 0:1], scale=-1.0,
-                accum_out=row_sums[head][:, tile_index : tile_index + 1],
+                accum_out=row_sums[step // 2][:, step % 2 : step % 2 + 1],
             )
             probs[step] = e_rows
 
@@ -219,89 +235,123 @@ def tile_selfattention_pb_t_kernel(tc, q_rot, k_rot, v, v1, lamb1, lamb2, wproj,
             probs_grouped[step] = grouped
 
         def quantise_probabilities(step):
-            head, tile_index = divmod(step, TILES)
-            if tile_index == 0:
-                e_codes[head] = heads.tile([P, TILES, PASSES, P], U32, name="e_codes", align_bytes=64)
-                e_scales[head] = heads.tile([P, TILES, PASSES, P], U8, name="e_scales", align_bytes=64)
+            if step % 2 == 0:
+                e_codes[step // 2] = steps.tile([P, 2, PASSES, P], U32, name="e_codes", bufs=PV_LAG // 2, align_bytes=64)
+                e_scales[step // 2] = steps.tile([P, 2, PASSES, P], U8, name="e_scales", bufs=PV_LAG // 2, align_bytes=64)
             nc.vector.quantize_mx(
-                out=e_codes[head][:, tile_index, :, :].rearrange("p g q -> p (g q)").bitcast(FP8X4),
-                scales=e_scales[head][:, tile_index, :, :].rearrange("p g q -> p (g q)"),
+                out=e_codes[step // 2][:, step % 2, :, :].rearrange("p g q -> p (g q)").bitcast(FP8X4),
+                scales=e_scales[step // 2][:, step % 2, :, :].rearrange("p g q -> p (g q)"),
                 in_=probs_grouped[step][:].rearrange("p g q t -> p (g q t)"),
             )
 
+        inverses = {}
         y_rows = {}
+        y_grouped = {}
         y_codes = {}
         y_scales = {}
 
         def attend(pair):
-            head, pair_in_head = divmod(pair, TILES // 2)
-            b, h = divmod(head, H)
-            first = 2 * pair_in_head
-            if h == 0 and pair_in_head == 0:
-                y_rows[b] = heads.tile([P, TILES, HD], BF16, name="y_rows")
-            inverse = steps.tile([P, 2], F32, name="inverse")
-            nc.vector.reciprocal(out=inverse[:], in_=row_sums[head][:, first : first + 2])
+            b, h, first_tile = place(2 * pair)
             bank = psum_other.tile([P, 2, D], F32, name="other_bank")
             for i in range(2):
                 for g in range(PASSES):
                     nc.tensor.matmul_mx(
                         out=bank[:, i, :],
-                        lhsT=e_codes[head][:, first + i, g, :].bitcast(FP8X4),
-                        lhsT_scale=e_scales[head][:, first + i, g, :],
-                        rhs=vm_codes[head][:, g, :].bitcast(FP8X4),
-                        rhs_scale=vm_scales[head][:, g, :],
+                        lhsT=e_codes[pair][:, i, g, :].bitcast(FP8X4),
+                        lhsT_scale=e_scales[pair][:, i, g, :],
+                        rhs=vm_codes[(b, h)][:, g, :].bitcast(FP8X4),
+                        rhs_scale=vm_scales[(b, h)][:, g, :],
                         start=(g == 0),
                         stop=(g == PASSES - 1),
                     )
+            other_banks[("attend", pair)] = bank
+
+        def invert_row_sums(pair):
+            inverses[pair] = steps.tile([P, 2], F32, name="inverse")
+            nc.vector.reciprocal(out=inverses[pair][:], in_=row_sums[pair][:])
+
+        def normalise(pair):
+            quad, h = divmod(pair, H)
+            if h == 0:
+                y_rows[quad] = steps.tile([P, 2, HD], BF16, name="y_rows")
             for i in range(2):
                 nc.vector.tensor_scalar(
-                    out=y_rows[b][:, first + i, h * D : (h + 1) * D], in0=bank[:, i, :],
-                    scalar1=inverse[:, i : i + 1], scalar2=None, op0=ALU.mult,
+                    out=y_rows[quad][:, i, h * D : (h + 1) * D], in0=other_banks[("attend", pair)][:, i, :],
+                    scalar1=inverses[pair][:, i : i + 1], scalar2=None, op0=ALU.mult,
                 )
 
-        def flip_outputs(out_pair):
-            b, pair_in_batch = divmod(out_pair, TILES // 2)
-            first = 2 * pair_in_batch
+        def flip_outputs(quad):
             bank = psum_other.tile([P, 2, PACK, P], BF16, name="other_bank")
             for i in range(2):
                 for t in range(PACK):
-                    nc.tensor.transpose(bank[:, i, t, :], y_rows[b][:, first + i, t * P : (t + 1) * P], ident_bf[:])
+                    nc.tensor.transpose(bank[:, i, t, :], y_rows[quad][:, i, t * P : (t + 1) * P], ident_bf[:])
+            other_banks[("y", quad)] = bank
+
+        def group_outputs(quad):
             grouped = steps.tile([P, 2, P, PACK], BF16, name="y_grouped", align_bytes=64)
-            nc.vector.tensor_copy(out=grouped[:], in_=bank[:].rearrange("p i t q -> p i q t"))
+            nc.vector.tensor_copy(out=grouped[:], in_=other_banks[("y", quad)][:].rearrange("p i t q -> p i q t"))
+            y_grouped[quad] = grouped
+
+        def quantise_outputs(quad):
             codes = steps.tile([P, 2, P], U32, name="y_codes", align_bytes=64)
             scales = steps.tile([P, 2, P], U8, name="y_scales", align_bytes=64)
             nc.vector.quantize_mx(
                 out=codes[:].rearrange("p i q -> p (i q)").bitcast(FP8X4),
                 scales=scales[:].rearrange("p i q -> p (i q)"),
-                in_=grouped[:].rearrange("p i q t -> p (i q t)"),
+                in_=y_grouped[quad][:].rearrange("p i q t -> p (i q t)"),
             )
-            y_codes[out_pair] = codes
-            y_scales[out_pair] = scales
+            y_codes[quad] = codes
+            y_scales[quad] = scales
 
-        def project(out_pair):
-            b, pair_in_batch = divmod(out_pair, TILES // 2)
-            g, t_first = divmod(2 * pair_in_batch, PACK)
+        def project(quad):
             bank = psum_other.tile([P, 2, C], F32, name="other_bank")
             for i in range(2):
                 nc.tensor.matmul_mx(
                     out=bank[:, i, :],
-                    lhsT=y_codes[out_pair][:, i, :].bitcast(FP8X4),
-                    lhsT_scale=y_scales[out_pair][:, i, :],
+                    lhsT=y_codes[quad][:, i, :].bitcast(FP8X4),
+                    lhsT_scale=y_scales[quad][:, i, :],
                     rhs=w_codes[:].bitcast(FP8X4),
                     rhs_scale=w_scales[:],
                     start=True,
                     stop=True,
                 )
+            other_banks[("out", quad)] = bank
+
+        def store_result(quad):
+            b, h, first_tile = place(4 * quad)
+            g, t_first = divmod(first_tile, PACK)
             result = steps.tile([P, 2, C], F32, name="result")
-            nc.scalar.copy(out=result[:], in_=bank[:])
+            nc.scalar.copy(out=result[:], in_=other_banks[("out", quad)][:])
             tokens_of_pass = out[b, g * K_PASS : (g + 1) * K_PASS, :].rearrange("(p t) c -> p t c", t=PACK)
             nc.sync.dma_start(out=tokens_of_pass[:, t_first : t_first + 2, :], in_=result[:])
 
+        for unit in range(FLIPS_AHEAD):
+            flip_half_head(unit)
+            keep_half_head(unit)
+        nc.vector.tensor_copy(out=lam1[:], in_=lam1_bf[:])
+        nc.vector.tensor_copy(out=lam2[:], in_=lam2_bf[:])
+
+        def due(r, lag, period, count):
+            index, off_beat = divmod(r - lag, period)
+            return index if off_beat == 0 and 0 <= index < count else None
+
         for r in range(ROUNDS):
-            next_batch = r // (H * TILES) + 1
-            if r % (H * TILES) == 0 and next_batch < B:
-                load_batch(next_batch)
-            next_head = r // TILES + 1
+            b_now, r_in_batch = divmod(r, STEPS_PER_BATCH)
+            if r_in_batch == TILES and b_now + 2 < B:
+                load_batch(b_now + 2)
+
+            unit = due(r - 1, -2 * FLIPS_AHEAD, 2, B * len(FLIP_ORDER))
+            if unit is not None and unit >= FLIPS_AHEAD:
+                keep_half_head(unit)
+            pair = due(r - 1, PV_LAG, 2, PAIRS)
+            if pair is not None:
+                normalise(pair)
+            grouped_quad = due(r - 1, Y_LAG, 4, QUADS)
+            if grouped_quad is not None:
+                group_outputs(grouped_quad)
+            quad = due(r - 1, OUT_LAG, 4, QUADS)
+            if quad is not None:
+                store_result(quad)
 
             flipping = 0 <= r - FLIP_LAG < STEPS
             if flipping:
@@ -315,25 +365,38 @@ def tile_selfattention_pb_t_kernel(tc, q_rot, k_rot, v, v1, lamb1, lamb2, wproj,
                             e_flipped[:, c, :], probs[r - FLIP_LAG][:, c * P : (c + 1) * P], ident_bf[:]
                         )
             if r < STEPS:
-                scale_and_bound(r)
+                scale_and_bound(r, 0)
+            if 0 <= r - QUANT_LAG < STEPS:
+                quantise_probabilities(r - QUANT_LAG)
+            if grouped_quad is not None:
+                quantise_outputs(grouped_quad)
+            pair = due(r, PV_LAG, 2, PAIRS)
+            if pair is not None:
+                invert_row_sums(pair)
+            if r < STEPS:
+                scale_and_bound(r, 1)
             if flipping:
                 group_probabilities(r - FLIP_LAG, e_flipped)
             if r < STEPS:
                 exponentials(r)
-            if 0 <= r - QUANT_LAG < STEPS:
-                quantise_probabilities(r - QUANT_LAG)
 
-            if r % 4 < HALVES and next_head < HEADS:
-                flip_half_head("k" if r % TILES < 4 else "q", next_head, r % 4)
+            unit = due(r, -2 * FLIPS_AHEAD, 2, B * len(FLIP_ORDER))
+            if unit is not None and unit >= FLIPS_AHEAD:
+                flip_half_head(unit)
             if r == W_ROUND:
                 prepare_weights()
-            if r % 4 == 2 and r < STEPS:
-                mix_values(r // TILES, (r % TILES) // 4)
-            if (r + 1 - PV_LAG) % TILES == 0 and 0 <= (r + 1 - PV_LAG) // TILES < HEADS:
-                quantise_values((r + 1 - PV_LAG) // TILES)
-            if (r - PV_LAG) % 2 == 0 and 0 <= (r - PV_LAG) // 2 < PAIRS:
-                attend((r - PV_LAG) // 2)
-            if (r - Y_LAG) % 4 == 0 and 0 <= (r - Y_LAG) // 4 < OUT_PAIRS:
-                flip_outputs((r - Y_LAG) // 4)
-            if (r - OUT_LAG) % 4 == 0 and 0 <= (r - OUT_LAG) // 4 < OUT_PAIRS:
-                project((r - OUT_LAG) // 4)
+            if pair is not None:
+                attend(pair)
+            quad = due(r, Y_LAG, 4, QUADS)
+            if quad is not None:
+                flip_outputs(quad)
+            quad = due(r, OUT_LAG, 4, QUADS)
+            if quad is not None:
+                project(quad)
+
+            if r < STEPS and 0 <= r_in_batch - MIX_ROUND < H * PASSES:
+                scale_second_values(b_now, *divmod(r_in_batch - MIX_ROUND, PASSES))
+            if r < STEPS and 0 <= r_in_batch - MIX_ROUND - 2 < H * PASSES:
+                mix_values(b_now, *divmod(r_in_batch - MIX_ROUND - 2, PASSES))
+            if r < STEPS and r_in_batch in (PV_LAG - 1, PV_LAG + 1):
+                quantise_values(b_now, (r_in_batch - PV_LAG + 1) // 2)

@@ -30,9 +30,9 @@ PAIRS = STEPS // 2
 QUADS = STEPS // 4
 FLIP_LAG = 3
 QUANT_LAG = 5
-PV_LAG = 6
-Y_LAG = PV_LAG + 3
-OUT_LAG = Y_LAG + 2
+SPREAD_LAG = 7
+PV_LAG = 8
+OUT_LAG = PV_LAG + 5
 W_ROUND = 1
 MIX_ROUND = 0
 ROUNDS = 4 * (QUADS - 1) + OUT_LAG + 2
@@ -96,9 +96,9 @@ def tile_selfattention_pb_t_kernel(tc, q_rot, k_rot, v, v1, lamb1, lamb2, wproj,
 
         def scale_second_values(b, h, g):
             term = steps.tile([P, PACK, D], F32, name="second_term")
-            nc.scalar.activation(
-                out=term[:], in_=raw[("v1_raw", b)][:, g * PACK : (g + 1) * PACK, h * D : (h + 1) * D],
-                func=ACT.Copy, scale=lam2[:, 0:1],
+            nc.vector.tensor_scalar(
+                out=term[:], in0=raw[("v1_raw", b)][:, g * PACK : (g + 1) * PACK, h * D : (h + 1) * D],
+                scalar1=lam2[:, 0:1], scalar2=None, op0=ALU.mult,
             )
             second_terms[(b, h, g)] = term
 
@@ -174,10 +174,7 @@ def tile_selfattention_pb_t_kernel(tc, q_rot, k_rot, v, v1, lamb1, lamb2, wproj,
             name, h, half = FLIP_ORDER[k]
             target = flipped_words[(name, b)][:, h, half * BANK : (half + 1) * BANK]
             bank = other_banks[("flip", unit)]
-            if unit % 2 == 0:
-                nc.scalar.copy(out=target, in_=bank[:].rearrange("p j r -> p (j r)"))
-            else:
-                nc.vector.tensor_copy(out=target, in_=bank[:].rearrange("p j r -> p (j r)"))
+            nc.scalar.copy(out=target, in_=bank[:].rearrange("p j r -> p (j r)"))
 
         score_banks = {}
         negated_scores = {}
@@ -221,7 +218,7 @@ def tile_selfattention_pb_t_kernel(tc, q_rot, k_rot, v, v1, lamb1, lamb2, wproj,
 
         def exponentials(step):
             if step % 2 == 0:
-                row_sums[step // 2] = steps.tile([P, 2], F32, name="row_sums", bufs=PV_LAG // 2 + 2)
+                row_sums[step // 2] = steps.tile([P, 2], F32, name="row_sums", bufs=PV_LAG // 2 + 1)
             e_rows = steps.tile([P, T], BF16, name="e_rows", bufs=FLIP_LAG + 2)
             nc.scalar.activation(
                 out=e_rows[:], in_=negated_scores[step][:], func=ACT.Exp, bias=biases[step][:, 0:1], scale=-1.0,
@@ -245,52 +242,58 @@ def tile_selfattention_pb_t_kernel(tc, q_rot, k_rot, v, v1, lamb1, lamb2, wproj,
             )
 
         inverses = {}
-        y_rows = {}
+        spread_inverses = {}
         y_grouped = {}
         y_codes = {}
         y_scales = {}
 
-        def attend(pair):
-            b, h, first_tile = place(2 * pair)
-            bank = psum_other.tile([P, 2, D], F32, name="other_bank")
-            for i in range(2):
+        def invert_row_sums(pair):
+            inverses[pair] = steps.tile([P, 2], F32, name="inverse", bufs=4)
+            nc.vector.reciprocal(out=inverses[pair][:], in_=row_sums[pair][:])
+
+        def spread_row_sums(quad):
+            bank = psum_other.tile([P, 2 * H, P], F32, name="other_bank")
+            for h in range(H):
+                for i in range(2):
+                    nc.tensor.transpose(
+                        bank[:, 2 * h + i, :], inverses[H * quad + h][:, i : i + 1].to_broadcast([P, P]), ident_f32[:]
+                    )
+            other_banks[("spread", quad)] = bank
+
+        def keep_row_sums(quad):
+            spread = steps.tile([P, H, 2, P], F32, name="spread")
+            nc.vector.tensor_copy(
+                out=spread[:].rearrange("p h i q -> p (h i q)"),
+                in_=other_banks[("spread", quad)][:].rearrange("p c q -> p (c q)"),
+            )
+            spread_inverses[quad] = spread
+
+        def attend(quad, i):
+            b, h_first, first_tile = place(4 * quad)
+            bank = psum_other.tile([P, PACK, P], F32, name="other_bank")
+            for t in range(PACK):
+                h, block = divmod(t, D // P)
                 for g in range(PASSES):
                     nc.tensor.matmul_mx(
-                        out=bank[:, i, :],
-                        lhsT=e_codes[pair][:, i, g, :].bitcast(FP8X4),
-                        lhsT_scale=e_scales[pair][:, i, g, :],
-                        rhs=vm_codes[(b, h)][:, g, :].bitcast(FP8X4),
-                        rhs_scale=vm_scales[(b, h)][:, g, :],
+                        out=bank[:, t, :],
+                        lhsT=vm_codes[(b, h)][:, g, block * P : (block + 1) * P].bitcast(FP8X4),
+                        lhsT_scale=vm_scales[(b, h)][:, g, block * P : (block + 1) * P],
+                        rhs=e_codes[H * quad + h][:, i, g, :].bitcast(FP8X4),
+                        rhs_scale=e_scales[H * quad + h][:, i, g, :],
                         start=(g == 0),
                         stop=(g == PASSES - 1),
                     )
-            other_banks[("attend", pair)] = bank
+            other_banks[("attend", quad, i)] = bank
 
-        def invert_row_sums(pair):
-            inverses[pair] = steps.tile([P, 2], F32, name="inverse")
-            nc.vector.reciprocal(out=inverses[pair][:], in_=row_sums[pair][:])
-
-        def normalise(pair):
-            quad, h = divmod(pair, H)
-            if h == 0:
-                y_rows[quad] = steps.tile([P, 2, HD], BF16, name="y_rows")
-            for i in range(2):
-                nc.vector.tensor_scalar(
-                    out=y_rows[quad][:, i, h * D : (h + 1) * D], in0=other_banks[("attend", pair)][:, i, :],
-                    scalar1=inverses[pair][:, i : i + 1], scalar2=None, op0=ALU.mult,
-                )
-
-        def flip_outputs(quad):
-            bank = psum_other.tile([P, 2, PACK, P], BF16, name="other_bank")
-            for i in range(2):
-                for t in range(PACK):
-                    nc.tensor.transpose(bank[:, i, t, :], y_rows[quad][:, i, t * P : (t + 1) * P], ident_bf[:])
-            other_banks[("y", quad)] = bank
-
-        def group_outputs(quad):
-            grouped = steps.tile([P, 2, P, PACK], BF16, name="y_grouped", align_bytes=64)
-            nc.vector.tensor_copy(out=grouped[:], in_=other_banks[("y", quad)][:].rearrange("p i t q -> p i q t"))
-            y_grouped[quad] = grouped
+        def normalise(quad, i):
+            if i == 0:
+                y_grouped[quad] = steps.tile([P, 2, P, PACK], BF16, name="y_grouped", align_bytes=64)
+            nc.vector.tensor_tensor(
+                out=y_grouped[quad][:, i, :, :].rearrange("p q (h e) -> p q h e", h=H),
+                in0=other_banks[("attend", quad, i)][:].rearrange("p (h e) q -> p q h e", h=H),
+                in1=spread_inverses[quad][:, :, i, :].rearrange("p h q -> p q h").unsqueeze(3).to_broadcast([P, P, H, D // P]),
+                op=ALU.mult,
+            )
 
         def quantise_outputs(quad):
             codes = steps.tile([P, 2, P], U32, name="y_codes", align_bytes=64)
@@ -335,6 +338,12 @@ def tile_selfattention_pb_t_kernel(tc, q_rot, k_rot, v, v1, lamb1, lamb2, wproj,
             index, off_beat = divmod(r - lag, period)
             return index if off_beat == 0 and 0 <= index < count else None
 
+        def mixing_rounds(b, chunk):
+            if b == 0:
+                return chunk, chunk + 2
+            start = (b - 1) * STEPS_PER_BATCH + 4 * chunk
+            return start + 8, start + 10
+
         for r in range(ROUNDS):
             b_now, r_in_batch = divmod(r, STEPS_PER_BATCH)
             if r_in_batch == TILES and b_now + 2 < B:
@@ -343,12 +352,12 @@ def tile_selfattention_pb_t_kernel(tc, q_rot, k_rot, v, v1, lamb1, lamb2, wproj,
             unit = due(r - 1, -2 * FLIPS_AHEAD, 2, B * len(FLIP_ORDER))
             if unit is not None and unit >= FLIPS_AHEAD:
                 keep_half_head(unit)
-            pair = due(r - 1, PV_LAG, 2, PAIRS)
-            if pair is not None:
-                normalise(pair)
-            grouped_quad = due(r - 1, Y_LAG, 4, QUADS)
-            if grouped_quad is not None:
-                group_outputs(grouped_quad)
+            quad = due(r - 1, SPREAD_LAG, 4, QUADS)
+            if quad is not None:
+                keep_row_sums(quad)
+            attended = due(r - 1, PV_LAG, 2, PAIRS)
+            if attended is not None:
+                normalise(*divmod(attended, 2))
             quad = due(r - 1, OUT_LAG, 4, QUADS)
             if quad is not None:
                 store_result(quad)
@@ -368,11 +377,12 @@ def tile_selfattention_pb_t_kernel(tc, q_rot, k_rot, v, v1, lamb1, lamb2, wproj,
                 scale_and_bound(r, 0)
             if 0 <= r - QUANT_LAG < STEPS:
                 quantise_probabilities(r - QUANT_LAG)
-            if grouped_quad is not None:
-                quantise_outputs(grouped_quad)
-            pair = due(r, PV_LAG, 2, PAIRS)
-            if pair is not None:
-                invert_row_sums(pair)
+            if attended is not None and attended % 2 == 1:
+                quantise_outputs(attended // 2)
+            quad = due(r, SPREAD_LAG - 1, 4, QUADS)
+            if quad is not None:
+                for h in range(H):
+                    invert_row_sums(H * quad + h)
             if r < STEPS:
                 scale_and_bound(r, 1)
             if flipping:
@@ -385,18 +395,22 @@ def tile_selfattention_pb_t_kernel(tc, q_rot, k_rot, v, v1, lamb1, lamb2, wproj,
                 flip_half_head(unit)
             if r == W_ROUND:
                 prepare_weights()
-            if pair is not None:
-                attend(pair)
-            quad = due(r, Y_LAG, 4, QUADS)
+            quad = due(r, SPREAD_LAG, 4, QUADS)
             if quad is not None:
-                flip_outputs(quad)
+                spread_row_sums(quad)
+            attending = due(r, PV_LAG, 2, PAIRS)
+            if attending is not None:
+                attend(*divmod(attending, 2))
             quad = due(r, OUT_LAG, 4, QUADS)
             if quad is not None:
                 project(quad)
 
-            if r < STEPS and 0 <= r_in_batch - MIX_ROUND < H * PASSES:
-                scale_second_values(b_now, *divmod(r_in_batch - MIX_ROUND, PASSES))
-            if r < STEPS and 0 <= r_in_batch - MIX_ROUND - 2 < H * PASSES:
-                mix_values(b_now, *divmod(r_in_batch - MIX_ROUND - 2, PASSES))
-            if r < STEPS and r_in_batch in (PV_LAG - 1, PV_LAG + 1):
-                quantise_values(b_now, (r_in_batch - PV_LAG + 1) // 2)
+            for b in range(B):
+                for chunk in range(H * PASSES):
+                    first_round, second_round = mixing_rounds(b, chunk)
+                    if r == first_round:
+                        scale_second_values(b, *divmod(chunk, PASSES))
+                    if r == second_round:
+                        mix_values(b, *divmod(chunk, PASSES))
+            if r < STEPS and 0 <= r_in_batch - (PV_LAG - H) < H:
+                quantise_values(b_now, r_in_batch - (PV_LAG - H))

@@ -22,114 +22,135 @@ TILES = T // P
 BANK = 512
 HALVES = T // BANK
 WORDS = D // 2
+BLOCKS = D // P
 SCALE = 1.0 / 16.0
 
-STEPS_PER_BATCH = H * TILES
-STEPS = B * STEPS_PER_BATCH
-PAIRS = STEPS // 2
-QUADS = STEPS // 4
+QUAD = 2 * H
+STEPS_PER_ENTRY = H * TILES
+STEPS = B * STEPS_PER_ENTRY
+QUADS = STEPS // QUAD
+
 FLIP_LAG = 3
 QUANT_LAG = 5
 SPREAD_LAG = 7
 PV_LAG = 8
 OUT_LAG = PV_LAG + 5
+ROUNDS = QUAD * (QUADS - 1) + OUT_LAG + 2
 W_ROUND = 1
-MIX_ROUND = 0
-ROUNDS = 4 * (QUADS - 1) + OUT_LAG + 2
+
 FLIP_ORDER = (
     ("k", 0, 0), ("k", 0, 1), ("q", 0, 0), ("k", 1, 0), ("k", 1, 1), ("q", 1, 0), ("q", 0, 1), ("q", 1, 1),
 )
+FLIP_UNITS = B * len(FLIP_ORDER)
 FLIPS_AHEAD = 6
+FLIP_PERIOD = STEPS_PER_ENTRY // len(FLIP_ORDER)
+
+CHUNKS = H * PASSES
+MIX_LEAD = 8
+MIX_GAP = 2
 
 FLOPS = 2 * B * H * T * T * D * 2 + 2 * B * T * HD * C
+
+
+def due(r, lag, period, count):
+    index, off_beat = divmod(r - lag, period)
+    return index if off_beat == 0 and 0 <= index < count else None
+
+
+def place(step):
+    b, rest = divmod(step, STEPS_PER_ENTRY)
+    j, rest = divmod(rest, QUAD)
+    h, i = divmod(rest, 2)
+    return b, h, 2 * j + i
+
+
+def mixing_rounds(b, chunk):
+    first = chunk if b == 0 else b * STEPS_PER_ENTRY - MIX_LEAD + QUAD * chunk
+    return first, first + MIX_GAP
 
 
 def tile_selfattention_pb_t_kernel(tc, q_rot, k_rot, v, v1, lamb1, lamb2, wproj, out):
     nc = tc.nc
     with ExitStack() as ctx:
         const = ctx.enter_context(tc.tile_pool(name="const", bufs=1))
-        loads = ctx.enter_context(tc.tile_pool(name="loads", bufs=2))
-        batches = ctx.enter_context(tc.tile_pool(name="batches", bufs=2))
-        steps = ctx.enter_context(tc.tile_pool(name="steps", bufs=3))
+        entries = ctx.enter_context(tc.tile_pool(name="entries", bufs=2))
+        rounds = ctx.enter_context(tc.tile_pool(name="rounds", bufs=3))
         psum_scores = ctx.enter_context(tc.psum_pool(name="psum_scores", bufs=3))
         psum_flips = ctx.enter_context(tc.psum_pool(name="psum_flips", bufs=2))
-        psum_other = ctx.enter_context(tc.psum_pool(name="psum_other", bufs=3))
+        psum_spare = ctx.enter_context(tc.psum_pool(name="psum_spare", bufs=3))
         ctx.enter_context(tc.manual_schedule())
+
+        kept = {}
 
         ident_bf = const.tile([P, P], BF16)
         make_identity(nc, ident_bf[:])
         ident_f32 = const.tile([P, P], F32)
         make_identity(nc, ident_f32[:])
 
-        raw = {}
-
         def load_tokens(name, source, b):
-            tokens = loads.tile([P, TILES, HD], BF16, name=name)
+            tokens = entries.tile([P, TILES, HD], BF16, name=name)
             for g in range(PASSES):
                 nc.sync.dma_start(
                     out=tokens[:, g * PACK : (g + 1) * PACK, :].rearrange("p t f -> p (t f)"),
                     in_=source[b, g * K_PASS : (g + 1) * K_PASS].rearrange("(p t) h d -> p (t h d)", p=P),
                 )
-            raw[(name, b)] = tokens
+            kept[(name, b)] = tokens
 
-        def load_batch(b):
-            load_tokens("k_raw", k_rot, b)
-            load_tokens("q_raw", q_rot, b)
-            load_tokens("v_raw", v, b)
-            load_tokens("v1_raw", v1, b)
+        def load_entry(b):
+            load_tokens("k", k_rot, b)
+            load_tokens("q", q_rot, b)
+            load_tokens("v", v, b)
+            load_tokens("v1", v1, b)
 
         lam1_bf = const.tile([P, 1], BF16)
         nc.sync.dma_start(out=lam1_bf[:], in_=lamb1.partition_broadcast(P))
         lam2_bf = const.tile([P, 1], BF16)
         nc.sync.dma_start(out=lam2_bf[:], in_=lamb2.partition_broadcast(P))
-        load_batch(0)
+        load_entry(0)
         w_raw = const.tile([P, C // P, HD], BF16)
         nc.sync.dma_start(out=w_raw[:], in_=wproj.rearrange("(o p) k -> p o k", p=P))
-        load_batch(1)
+        load_entry(1)
         lam1 = const.tile([P, 1], F32)
         lam2 = const.tile([P, 1], F32)
 
-        second_terms = {}
-        vm_grouped = {}
-        vm_codes = {}
-        vm_scales = {}
-
         def scale_second_values(b, h, g):
-            term = steps.tile([P, PACK, D], F32, name="second_term")
+            term = rounds.tile([P, PACK, D], F32, name="second_term")
             nc.vector.tensor_scalar(
-                out=term[:], in0=raw[("v1_raw", b)][:, g * PACK : (g + 1) * PACK, h * D : (h + 1) * D],
+                out=term[:], in0=kept[("v1", b)][:, g * PACK : (g + 1) * PACK, h * D : (h + 1) * D],
                 scalar1=lam2[:, 0:1], scalar2=None, op0=ALU.mult,
             )
-            second_terms[(b, h, g)] = term
+            kept[("second_term", b, h, g)] = term
 
         def mix_values(b, h, g):
             if g == 0:
-                vm_grouped[(b, h)] = steps.tile([P, PASSES, D, PACK], BF16, name="vm_grouped", align_bytes=64)
+                kept[("vm_grouped", b, h)] = entries.tile(
+                    [P, PASSES, D, PACK], BF16, name="vm_grouped%d" % h, align_bytes=64
+                )
             nc.vector.scalar_tensor_tensor(
-                out=vm_grouped[(b, h)][:, g, :, :],
-                in0=raw[("v_raw", b)][:, g * PACK : (g + 1) * PACK, h * D : (h + 1) * D].rearrange("p t d -> p d t"),
+                out=kept[("vm_grouped", b, h)][:, g, :, :],
+                in0=kept[("v", b)][:, g * PACK : (g + 1) * PACK, h * D : (h + 1) * D].rearrange("p t d -> p d t"),
                 scalar=lam1[:, 0:1],
-                in1=second_terms[(b, h, g)][:].rearrange("p t d -> p d t"),
+                in1=kept[("second_term", b, h, g)][:].rearrange("p t d -> p d t"),
                 op0=ALU.mult,
                 op1=ALU.add,
             )
 
         def quantise_values(b, h):
-            codes = batches.tile([P, PASSES, D], U32, name="vm_codes%d" % h, align_bytes=64)
-            scales = batches.tile([P, PASSES, D], U8, name="vm_scales%d" % h, align_bytes=64)
+            codes = entries.tile([P, PASSES, D], U32, name="vm_codes%d" % h, align_bytes=64)
+            scales = entries.tile([P, PASSES, D], U8, name="vm_scales%d" % h, align_bytes=64)
             nc.vector.quantize_mx(
                 out=codes[:].rearrange("p g d -> p (g d)").bitcast(FP8X4),
                 scales=scales[:].rearrange("p g d -> p (g d)"),
-                in_=vm_grouped[(b, h)][:].rearrange("p g d t -> p (g d t)"),
+                in_=kept[("vm_grouped", b, h)][:].rearrange("p g d t -> p (g d t)"),
             )
-            vm_codes[(b, h)] = codes
-            vm_scales[(b, h)] = scales
+            kept[("vm_codes", b, h)] = codes
+            kept[("vm_scales", b, h)] = scales
 
         w_codes = const.tile([P, C], U32, align_bytes=64)
         w_scales = const.tile([P, C], U8, align_bytes=64)
 
         def prepare_weights():
-            w_flipped = psum_other.tile([P, PACK, C], BF16, name="other_bank")
+            w_flipped = psum_spare.tile([P, PACK, C], BF16, name="spare_bank")
             for o in range(C // P):
                 for t in range(PACK):
                     nc.tensor.transpose(
@@ -142,275 +163,250 @@ def tile_selfattention_pb_t_kernel(tc, q_rot, k_rot, v, v1, lamb1, lamb2, wproj,
                 in_=w_grouped[:].rearrange("p c t -> p (c t)"),
             )
 
-        flipped_words = {}
-        flipped_pairs = {}
-
-        other_banks = {}
-
-        def flip_half_head(unit):
+        def transpose_half_head(unit):
             b, k = divmod(unit, len(FLIP_ORDER))
             name, h, half = FLIP_ORDER[k]
             words = (
-                raw[(name + "_raw", b)][:]
+                kept[(name, b)][:]
                 .rearrange("p c f -> p (c f)")
                 .bitcast(F32)
                 .rearrange("p (c w) -> p c w", c=TILES)
             )
-            if (name, b) not in flipped_words:
-                flipped = batches.tile([P, H, T], F32, name=name + "_flipped")
-                flipped_words[(name, b)] = flipped
-                flipped_pairs[(name, b)] = (
-                    flipped[:].rearrange("p h n -> p (h n)").bitcast(BF16).rearrange("p (h n e) -> p h n e", h=H, e=2)
-                )
-            bank = psum_other.tile([P, PACK, P], F32, name="other_bank")
+            bank = psum_spare.tile([P, PACK, P], F32, name="spare_bank")
             for j in range(PACK):
                 nc.tensor.transpose(
                     bank[:, j, :], words[:, half * PACK + j, h * WORDS : (h + 1) * WORDS], ident_f32[:]
                 )
-            other_banks[("flip", unit)] = bank
+            kept[("flip_bank", unit)] = bank
 
-        def keep_half_head(unit):
+        def copy_half_head(unit):
             b, k = divmod(unit, len(FLIP_ORDER))
             name, h, half = FLIP_ORDER[k]
-            target = flipped_words[(name, b)][:, h, half * BANK : (half + 1) * BANK]
-            bank = other_banks[("flip", unit)]
-            nc.scalar.copy(out=target, in_=bank[:].rearrange("p j r -> p (j r)"))
-
-        score_banks = {}
-        negated_scores = {}
-        first_mins = {}
-        biases = {}
-        row_sums = {}
-        probs = {}
-        probs_grouped = {}
-        e_codes = {}
-        e_scales = {}
-
-        def place(step):
-            b, rest = divmod(step, STEPS_PER_BATCH)
-            j, rest = divmod(rest, 2 * H)
-            h, i = divmod(rest, 2)
-            return b, h, 2 * j + i
+            if (name + "_words", b) not in kept:
+                flipped = entries.tile([P, H, T], F32, name=name + "_flipped")
+                kept[(name + "_words", b)] = flipped
+                kept[(name + "_pairs", b)] = (
+                    flipped[:].rearrange("p h n -> p (h n)").bitcast(BF16).rearrange("p (h n e) -> p h n e", h=H, e=2)
+                )
+            nc.scalar.copy(
+                out=kept[(name + "_words", b)][:, h, half * BANK : (half + 1) * BANK],
+                in_=kept[("flip_bank", unit)][:].rearrange("p j r -> p (j r)"),
+            )
 
         def score_matmul(step, half, parity):
             b, h, tile_index = place(step)
             if parity == 0:
-                score_banks[(step, half)] = psum_scores.tile([P, BANK], F32, name="score_bank")
+                kept[("scores", step, half)] = psum_scores.tile([P, BANK], F32, name="score_bank")
             nc.tensor.matmul(
-                score_banks[(step, half)][:],
-                lhsT=flipped_pairs[("q", b)][:, h, tile_index * P : (tile_index + 1) * P, parity],
-                rhs=flipped_pairs[("k", b)][:, h, half * BANK : (half + 1) * BANK, parity],
+                kept[("scores", step, half)][:],
+                lhsT=kept[("q_pairs", b)][:, h, tile_index * P : (tile_index + 1) * P, parity],
+                rhs=kept[("k_pairs", b)][:, h, half * BANK : (half + 1) * BANK, parity],
                 start=(parity == 0),
                 stop=(parity == 1),
             )
 
         def scale_and_bound(step, half):
             if half == 0:
-                negated_scores[step] = steps.tile([P, T], F32, name="negated")
-                first_mins[step] = steps.tile([P, 1], F32, name="first_min")
-                biases[step] = steps.tile([P, 1], F32, name="bias")
+                kept[("negated", step)] = rounds.tile([P, T], F32, name="negated")
+                kept[("first_min", step)] = rounds.tile([P, 1], F32, name="first_min")
+                kept[("bias", step)] = rounds.tile([P, 1], F32, name="bias")
             nc.vector.tensor_scalar(
-                out=negated_scores[step][:, half * BANK : (half + 1) * BANK], in0=score_banks[(step, half)][:],
-                scalar1=-SCALE, scalar2=(None if half == 0 else first_mins[step][:, 0:1]),
-                op0=ALU.mult, op1=ALU.min,
-                accum_out=(first_mins[step][:] if half == 0 else biases[step][:]),
+                out=kept[("negated", step)][:, half * BANK : (half + 1) * BANK],
+                in0=kept[("scores", step, half)][:],
+                scalar1=-SCALE,
+                scalar2=(None if half == 0 else kept[("first_min", step)][:, 0:1]),
+                op0=ALU.mult,
+                op1=ALU.min,
+                accum_out=(kept[("first_min", step)][:] if half == 0 else kept[("bias", step)][:]),
             )
 
         def exponentials(step):
-            if step % 2 == 0:
-                row_sums[step // 2] = steps.tile([P, 2], F32, name="row_sums", bufs=PV_LAG // 2 + 1)
-            e_rows = steps.tile([P, T], BF16, name="e_rows", bufs=FLIP_LAG + 2)
+            quad, slot = divmod(step, QUAD)
+            if slot == 0:
+                kept[("row_sums", quad)] = rounds.tile([P, QUAD], F32, name="row_sums")
+            e_rows = rounds.tile([P, T], BF16, name="e_rows", bufs=FLIP_LAG + 1)
             nc.scalar.activation(
-                out=e_rows[:], in_=negated_scores[step][:], func=ACT.Exp, bias=biases[step][:, 0:1], scale=-1.0,
-                accum_out=row_sums[step // 2][:, step % 2 : step % 2 + 1],
+                out=e_rows[:], in_=kept[("negated", step)][:], func=ACT.Exp,
+                bias=kept[("bias", step)][:, 0:1], scale=-1.0,
+                accum_out=kept[("row_sums", quad)][:, slot : slot + 1],
             )
-            probs[step] = e_rows
+            kept[("e_rows", step)] = e_rows
 
-        def group_probabilities(step, e_flipped):
-            grouped = steps.tile([P, PASSES, P, PACK], BF16, name="e_grouped", align_bytes=64)
-            nc.scalar.copy(out=grouped[:], in_=e_flipped[:].rearrange("p (g t) q -> p g q t", g=PASSES))
-            probs_grouped[step] = grouped
+        def transpose_probabilities(step, c):
+            if c == 0:
+                kept[("e_flipped", step)] = psum_flips.tile([P, TILES, P], BF16, name="e_flipped")
+            nc.tensor.transpose(
+                kept[("e_flipped", step)][:, c, :], kept[("e_rows", step)][:, c * P : (c + 1) * P], ident_bf[:]
+            )
+
+        def group_probabilities(step):
+            grouped = rounds.tile([P, PASSES, P, PACK], BF16, name="e_grouped", align_bytes=64)
+            nc.scalar.copy(out=grouped[:], in_=kept[("e_flipped", step)][:].rearrange("p (g t) q -> p g q t", g=PASSES))
+            kept[("e_grouped", step)] = grouped
 
         def quantise_probabilities(step):
-            if step % 2 == 0:
-                e_codes[step // 2] = steps.tile([P, 2, PASSES, P], U32, name="e_codes", bufs=PV_LAG // 2, align_bytes=64)
-                e_scales[step // 2] = steps.tile([P, 2, PASSES, P], U8, name="e_scales", bufs=PV_LAG // 2, align_bytes=64)
+            quad, slot = divmod(step, QUAD)
+            if slot == 0:
+                kept[("e_codes", quad)] = rounds.tile([P, QUAD, PASSES, P], U32, name="e_codes", align_bytes=64)
+                kept[("e_scales", quad)] = rounds.tile([P, QUAD, PASSES, P], U8, name="e_scales", align_bytes=64)
             nc.vector.quantize_mx(
-                out=e_codes[step // 2][:, step % 2, :, :].rearrange("p g q -> p (g q)").bitcast(FP8X4),
-                scales=e_scales[step // 2][:, step % 2, :, :].rearrange("p g q -> p (g q)"),
-                in_=probs_grouped[step][:].rearrange("p g q t -> p (g q t)"),
+                out=kept[("e_codes", quad)][:, slot, :, :].rearrange("p g q -> p (g q)").bitcast(FP8X4),
+                scales=kept[("e_scales", quad)][:, slot, :, :].rearrange("p g q -> p (g q)"),
+                in_=kept[("e_grouped", step)][:].rearrange("p g q t -> p (g q t)"),
             )
 
-        inverses = {}
-        spread_inverses = {}
-        y_grouped = {}
-        y_codes = {}
-        y_scales = {}
-
-        def invert_row_sums(pair):
-            inverses[pair] = steps.tile([P, 2], F32, name="inverse", bufs=4)
-            nc.vector.reciprocal(out=inverses[pair][:], in_=row_sums[pair][:])
+        def invert_row_sums(quad):
+            inverse = rounds.tile([P, QUAD], F32, name="inverse")
+            nc.vector.reciprocal(out=inverse[:], in_=kept[("row_sums", quad)][:])
+            kept[("inverse", quad)] = inverse
 
         def spread_row_sums(quad):
-            bank = psum_other.tile([P, 2 * H, P], F32, name="other_bank")
-            for h in range(H):
-                for i in range(2):
-                    nc.tensor.transpose(
-                        bank[:, 2 * h + i, :], inverses[H * quad + h][:, i : i + 1].to_broadcast([P, P]), ident_f32[:]
-                    )
-            other_banks[("spread", quad)] = bank
+            bank = psum_spare.tile([P, QUAD, P], F32, name="spare_bank")
+            for slot in range(QUAD):
+                nc.tensor.transpose(
+                    bank[:, slot, :], kept[("inverse", quad)][:, slot : slot + 1].to_broadcast([P, P]), ident_f32[:]
+                )
+            kept[("spread_bank", quad)] = bank
 
-        def keep_row_sums(quad):
-            spread = steps.tile([P, H, 2, P], F32, name="spread")
+        def copy_spread_row_sums(quad):
+            spread = rounds.tile([P, H, 2, P], F32, name="spread")
             nc.vector.tensor_copy(
                 out=spread[:].rearrange("p h i q -> p (h i q)"),
-                in_=other_banks[("spread", quad)][:].rearrange("p c q -> p (c q)"),
+                in_=kept[("spread_bank", quad)][:].rearrange("p c q -> p (c q)"),
             )
-            spread_inverses[quad] = spread
+            kept[("spread", quad)] = spread
 
         def attend(quad, i):
-            b, h_first, first_tile = place(4 * quad)
-            bank = psum_other.tile([P, PACK, P], F32, name="other_bank")
+            b = place(QUAD * quad)[0]
+            bank = psum_spare.tile([P, PACK, P], F32, name="spare_bank")
             for t in range(PACK):
-                h, block = divmod(t, D // P)
+                h, block = divmod(t, BLOCKS)
                 for g in range(PASSES):
                     nc.tensor.matmul_mx(
                         out=bank[:, t, :],
-                        lhsT=vm_codes[(b, h)][:, g, block * P : (block + 1) * P].bitcast(FP8X4),
-                        lhsT_scale=vm_scales[(b, h)][:, g, block * P : (block + 1) * P],
-                        rhs=e_codes[H * quad + h][:, i, g, :].bitcast(FP8X4),
-                        rhs_scale=e_scales[H * quad + h][:, i, g, :],
+                        lhsT=kept[("vm_codes", b, h)][:, g, block * P : (block + 1) * P].bitcast(FP8X4),
+                        lhsT_scale=kept[("vm_scales", b, h)][:, g, block * P : (block + 1) * P],
+                        rhs=kept[("e_codes", quad)][:, 2 * h + i, g, :].bitcast(FP8X4),
+                        rhs_scale=kept[("e_scales", quad)][:, 2 * h + i, g, :],
                         start=(g == 0),
                         stop=(g == PASSES - 1),
                     )
-            other_banks[("attend", quad, i)] = bank
+            kept[("y_bank", quad, i)] = bank
 
         def normalise(quad, i):
             if i == 0:
-                y_grouped[quad] = steps.tile([P, 2, P, PACK], BF16, name="y_grouped", align_bytes=64)
+                kept[("y_grouped", quad)] = rounds.tile([P, 2, P, PACK], BF16, name="y_grouped", align_bytes=64)
             nc.vector.tensor_tensor(
-                out=y_grouped[quad][:, i, :, :].rearrange("p q (h e) -> p q h e", h=H),
-                in0=other_banks[("attend", quad, i)][:].rearrange("p (h e) q -> p q h e", h=H),
-                in1=spread_inverses[quad][:, :, i, :].rearrange("p h q -> p q h").unsqueeze(3).to_broadcast([P, P, H, D // P]),
+                out=kept[("y_grouped", quad)][:, i, :, :].rearrange("p q (h e) -> p q h e", h=H),
+                in0=kept[("y_bank", quad, i)][:].rearrange("p (h e) q -> p q h e", h=H),
+                in1=kept[("spread", quad)][:, :, i, :].rearrange("p h q -> p q h").unsqueeze(3).to_broadcast([P, P, H, BLOCKS]),
                 op=ALU.mult,
             )
 
         def quantise_outputs(quad):
-            codes = steps.tile([P, 2, P], U32, name="y_codes", align_bytes=64)
-            scales = steps.tile([P, 2, P], U8, name="y_scales", align_bytes=64)
+            codes = rounds.tile([P, 2, P], U32, name="y_codes", align_bytes=64)
+            scales = rounds.tile([P, 2, P], U8, name="y_scales", align_bytes=64)
             nc.vector.quantize_mx(
                 out=codes[:].rearrange("p i q -> p (i q)").bitcast(FP8X4),
                 scales=scales[:].rearrange("p i q -> p (i q)"),
-                in_=y_grouped[quad][:].rearrange("p i q t -> p (i q t)"),
+                in_=kept[("y_grouped", quad)][:].rearrange("p i q t -> p (i q t)"),
             )
-            y_codes[quad] = codes
-            y_scales[quad] = scales
+            kept[("y_codes", quad)] = codes
+            kept[("y_scales", quad)] = scales
 
         def project(quad):
-            bank = psum_other.tile([P, 2, C], F32, name="other_bank")
+            bank = psum_spare.tile([P, 2, C], F32, name="spare_bank")
             for i in range(2):
                 nc.tensor.matmul_mx(
                     out=bank[:, i, :],
-                    lhsT=y_codes[quad][:, i, :].bitcast(FP8X4),
-                    lhsT_scale=y_scales[quad][:, i, :],
+                    lhsT=kept[("y_codes", quad)][:, i, :].bitcast(FP8X4),
+                    lhsT_scale=kept[("y_scales", quad)][:, i, :],
                     rhs=w_codes[:].bitcast(FP8X4),
                     rhs_scale=w_scales[:],
                     start=True,
                     stop=True,
                 )
-            other_banks[("out", quad)] = bank
+            kept[("out_bank", quad)] = bank
 
         def store_result(quad):
-            b, h, first_tile = place(4 * quad)
+            b, h, first_tile = place(QUAD * quad)
             g, t_first = divmod(first_tile, PACK)
-            result = steps.tile([P, 2, C], F32, name="result")
-            nc.scalar.copy(out=result[:], in_=other_banks[("out", quad)][:])
+            result = rounds.tile([P, 2, C], F32, name="result")
+            nc.scalar.copy(out=result[:], in_=kept[("out_bank", quad)][:])
             tokens_of_pass = out[b, g * K_PASS : (g + 1) * K_PASS, :].rearrange("(p t) c -> p t c", t=PACK)
             nc.sync.dma_start(out=tokens_of_pass[:, t_first : t_first + 2, :], in_=result[:])
 
         for unit in range(FLIPS_AHEAD):
-            flip_half_head(unit)
-            keep_half_head(unit)
+            transpose_half_head(unit)
+            copy_half_head(unit)
         nc.vector.tensor_copy(out=lam1[:], in_=lam1_bf[:])
         nc.vector.tensor_copy(out=lam2[:], in_=lam2_bf[:])
 
-        def due(r, lag, period, count):
-            index, off_beat = divmod(r - lag, period)
-            return index if off_beat == 0 and 0 <= index < count else None
-
-        def mixing_rounds(b, chunk):
-            if b == 0:
-                return chunk, chunk + 2
-            start = (b - 1) * STEPS_PER_BATCH + 4 * chunk
-            return start + 8, start + 10
-
         for r in range(ROUNDS):
-            b_now, r_in_batch = divmod(r, STEPS_PER_BATCH)
-            if r_in_batch == TILES and b_now + 2 < B:
-                load_batch(b_now + 2)
+            entry_now, r_in_entry = divmod(r, STEPS_PER_ENTRY)
+            if r_in_entry == STEPS_PER_ENTRY // 2 and entry_now + 2 < B:
+                load_entry(entry_now + 2)
 
-            unit = due(r - 1, -2 * FLIPS_AHEAD, 2, B * len(FLIP_ORDER))
-            if unit is not None and unit >= FLIPS_AHEAD:
-                keep_half_head(unit)
-            quad = due(r - 1, SPREAD_LAG, 4, QUADS)
+            late_unit = due(r - 1, 0, FLIP_PERIOD, FLIP_UNITS - FLIPS_AHEAD)
+            if late_unit is not None:
+                copy_half_head(FLIPS_AHEAD + late_unit)
+            quad = due(r - 1, SPREAD_LAG, QUAD, QUADS)
             if quad is not None:
-                keep_row_sums(quad)
-            attended = due(r - 1, PV_LAG, 2, PAIRS)
+                copy_spread_row_sums(quad)
+            attended = due(r - 1, PV_LAG, 2, 2 * QUADS)
             if attended is not None:
                 normalise(*divmod(attended, 2))
-            quad = due(r - 1, OUT_LAG, 4, QUADS)
+            quad = due(r - 1, OUT_LAG, QUAD, QUADS)
             if quad is not None:
                 store_result(quad)
 
             flipping = 0 <= r - FLIP_LAG < STEPS
-            if flipping:
-                e_flipped = psum_flips.tile([P, TILES, P], BF16, name="e_flipped")
             for piece in range(2 * HALVES):
                 if r < STEPS:
                     score_matmul(r, piece // 2, piece % 2)
                 if flipping:
-                    for c in (2 * piece, 2 * piece + 1):
-                        nc.tensor.transpose(
-                            e_flipped[:, c, :], probs[r - FLIP_LAG][:, c * P : (c + 1) * P], ident_bf[:]
-                        )
+                    transpose_probabilities(r - FLIP_LAG, 2 * piece)
+                    transpose_probabilities(r - FLIP_LAG, 2 * piece + 1)
+
             if r < STEPS:
                 scale_and_bound(r, 0)
             if 0 <= r - QUANT_LAG < STEPS:
                 quantise_probabilities(r - QUANT_LAG)
             if attended is not None and attended % 2 == 1:
                 quantise_outputs(attended // 2)
-            quad = due(r, SPREAD_LAG - 1, 4, QUADS)
+            quad = due(r, SPREAD_LAG - 1, QUAD, QUADS)
             if quad is not None:
-                for h in range(H):
-                    invert_row_sums(H * quad + h)
+                invert_row_sums(quad)
             if r < STEPS:
                 scale_and_bound(r, 1)
+
             if flipping:
-                group_probabilities(r - FLIP_LAG, e_flipped)
+                group_probabilities(r - FLIP_LAG)
             if r < STEPS:
                 exponentials(r)
 
-            unit = due(r, -2 * FLIPS_AHEAD, 2, B * len(FLIP_ORDER))
-            if unit is not None and unit >= FLIPS_AHEAD:
-                flip_half_head(unit)
+            late_unit = due(r, 0, FLIP_PERIOD, FLIP_UNITS - FLIPS_AHEAD)
+            if late_unit is not None:
+                transpose_half_head(FLIPS_AHEAD + late_unit)
             if r == W_ROUND:
                 prepare_weights()
-            quad = due(r, SPREAD_LAG, 4, QUADS)
+            quad = due(r, SPREAD_LAG, QUAD, QUADS)
             if quad is not None:
                 spread_row_sums(quad)
-            attending = due(r, PV_LAG, 2, PAIRS)
+            attending = due(r, PV_LAG, 2, 2 * QUADS)
             if attending is not None:
                 attend(*divmod(attending, 2))
-            quad = due(r, OUT_LAG, 4, QUADS)
+            quad = due(r, OUT_LAG, QUAD, QUADS)
             if quad is not None:
                 project(quad)
 
             for b in range(B):
-                for chunk in range(H * PASSES):
+                for chunk in range(CHUNKS):
                     first_round, second_round = mixing_rounds(b, chunk)
                     if r == first_round:
                         scale_second_values(b, *divmod(chunk, PASSES))
                     if r == second_round:
                         mix_values(b, *divmod(chunk, PASSES))
-            if r < STEPS and 0 <= r_in_batch - (PV_LAG - H) < H:
-                quantise_values(b_now, r_in_batch - (PV_LAG - H))
+            h = r_in_entry - (PV_LAG - H)
+            if r < STEPS and 0 <= h < H:
+                quantise_values(entry_now, h)

@@ -188,10 +188,15 @@ def tile_selfattention_pb_t_kernel(tc, q_rot, k_rot, v, v1, lamb1, lamb2, wproj,
                 kept[(name + "_pairs", b)] = (
                     flipped[:].rearrange("p h n -> p (h n)").bitcast(BF16).rearrange("p (h n e) -> p h n e", h=H, e=2)
                 )
-            nc.scalar.copy(
-                out=kept[(name + "_words", b)][:, h, half * BANK : (half + 1) * BANK],
-                in_=kept[("flip_bank", unit)][:].rearrange("p j r -> p (j r)"),
-            )
+            out = kept[(name + "_words", b)][:, h, half * BANK : (half + 1) * BANK]
+            bank = kept[("flip_bank", unit)]
+            if name == "k":
+                nc.scalar.copy(
+                    out=out.rearrange("p (u r e) -> p u r e", u=2, e=2),
+                    in_=bank[:].rearrange("p (u e) r -> p u r e", e=2),
+                )
+            else:
+                nc.scalar.copy(out=out, in_=bank[:].rearrange("p j r -> p (j r)"))
 
         def score_matmul(step, half, parity):
             b, h, tile_index = place(step)
@@ -234,14 +239,19 @@ def tile_selfattention_pb_t_kernel(tc, q_rot, k_rot, v, v1, lamb1, lamb2, wproj,
 
         def transpose_probabilities(step, c):
             if c == 0:
-                kept[("e_flipped", step)] = psum_flips.tile([P, TILES, P], BF16, name="e_flipped")
+                kept[("e_flipped", step)] = psum_flips.tile([P, 2 * PASSES, P], F32, name="e_flipped")
             nc.tensor.transpose(
-                kept[("e_flipped", step)][:, c, :], kept[("e_rows", step)][:, c * P : (c + 1) * P], ident_bf[:]
+                kept[("e_flipped", step)][:, c, :],
+                kept[("e_rows", step)][:].bitcast(F32)[:, c * P : (c + 1) * P],
+                ident_f32[:],
             )
 
         def group_probabilities(step):
             grouped = rounds.tile([P, PASSES, P, PACK], BF16, name="e_grouped", align_bytes=64)
-            nc.scalar.copy(out=grouped[:], in_=kept[("e_flipped", step)][:].rearrange("p (g t) q -> p g q t", g=PASSES))
+            nc.scalar.copy(
+                out=grouped[:].bitcast(F32),
+                in_=kept[("e_flipped", step)][:].rearrange("p (g u) q -> p g q u", g=PASSES),
+            )
             kept[("e_grouped", step)] = grouped
 
         def quantise_probabilities(step):
@@ -365,8 +375,7 @@ def tile_selfattention_pb_t_kernel(tc, q_rot, k_rot, v, v1, lamb1, lamb2, wproj,
                 if r < STEPS:
                     score_matmul(r, piece // 2, piece % 2)
                 if flipping:
-                    transpose_probabilities(r - FLIP_LAG, 2 * piece)
-                    transpose_probabilities(r - FLIP_LAG, 2 * piece + 1)
+                    transpose_probabilities(r - FLIP_LAG, piece)
 
             if r < STEPS:
                 scale_and_bound(r, 0)

@@ -115,10 +115,11 @@ def tile_selfattention_pb_t_kernel(tc, q_rot, k_rot, v, v1, lamb1, lamb2, wproj,
 
         def scale_second_values(b, h, g):
             term = rounds.tile([P, PACK, D], F32, name="second_term")
-            nc.vector.tensor_scalar(
-                out=term[:], in0=kept[("v1", b)][:, g * PACK : (g + 1) * PACK, h * D : (h + 1) * D],
-                scalar1=lam2[:, 0:1], scalar2=None, op0=ALU.mult,
-            )
+            for t in range(PACK):
+                nc.gpsimd.tensor_scalar(
+                    out=term[:, t, :], in0=kept[("v1", b)][:, g * PACK + t, h * D : (h + 1) * D],
+                    scalar1=lam2[:, 0:1], scalar2=0.0, op0=ALU.mult, op1=ALU.add,
+                )
             kept[("second_term", b, h, g)] = term
 
         def mix_values(b, h, g):

@@ -23,6 +23,7 @@ BANK = 512
 HALVES = T // BANK
 WORDS = D // 2
 BLOCKS = D // P
+QUARTER = D // 4
 SCALE = 1.0 / 16.0
 
 QUAD = 2 * H
@@ -114,10 +115,11 @@ def tile_selfattention_pb_t_kernel(tc, q_rot, k_rot, v, v1, lamb1, lamb2, wproj,
         lam2 = const.tile([P, 1], F32)
 
         def scale_second_values(b, h, g):
-            term = rounds.tile([P, PACK, D], F32, name="second_term")
-            for t in range(PACK):
+            term = rounds.tile([P, D, PACK], F32, name="second_term")
+            source = kept[("v1", b)][:, g * PACK : (g + 1) * PACK, h * D : (h + 1) * D].rearrange("p t d -> p d t")
+            for d in range(0, D, QUARTER):
                 nc.gpsimd.tensor_scalar(
-                    out=term[:, t, :], in0=kept[("v1", b)][:, g * PACK + t, h * D : (h + 1) * D],
+                    out=term[:, d : d + QUARTER, :], in0=source[:, d : d + QUARTER, :],
                     scalar1=lam2[:, 0:1], scalar2=0.0, op0=ALU.mult, op1=ALU.add,
                 )
             kept[("second_term", b, h, g)] = term
@@ -131,7 +133,7 @@ def tile_selfattention_pb_t_kernel(tc, q_rot, k_rot, v, v1, lamb1, lamb2, wproj,
                 out=kept[("vm_grouped", b, h)][:, g, :, :],
                 in0=kept[("v", b)][:, g * PACK : (g + 1) * PACK, h * D : (h + 1) * D].rearrange("p t d -> p d t"),
                 scalar=lam1[:, 0:1],
-                in1=kept[("second_term", b, h, g)][:].rearrange("p t d -> p d t"),
+                in1=kept[("second_term", b, h, g)][:],
                 op0=ALU.mult,
                 op1=ALU.add,
             )

@@ -114,29 +114,37 @@ def tile_selfattention_pb_t_kernel(tc, q_rot, k_rot, v, v1, lamb1, lamb2, wproj,
         lam1 = const.tile([P, 1], F32)
         lam2 = const.tile([P, 1], F32)
 
-        def scale_second_values(b, h, g):
-            term = rounds.tile([P, D, PACK], F32, name="second_term")
-            source = kept[("v1", b)][:, g * PACK : (g + 1) * PACK, h * D : (h + 1) * D].rearrange("p t d -> p d t")
+        def scale_values(name, factor, b, h, g):
+            term = rounds.tile([P, D, PACK], F32, name=name + "_term")
+            source = kept[(name, b)][:, g * PACK : (g + 1) * PACK, h * D : (h + 1) * D].rearrange("p t d -> p d t")
             for d in range(0, D, QUARTER):
                 nc.gpsimd.tensor_scalar(
                     out=term[:, d : d + QUARTER, :], in0=source[:, d : d + QUARTER, :],
-                    scalar1=lam2[:, 0:1], scalar2=0.0, op0=ALU.mult, op1=ALU.add,
+                    scalar1=factor[:, 0:1], scalar2=0.0, op0=ALU.mult, op1=ALU.add,
                 )
-            kept[("second_term", b, h, g)] = term
+            kept[(name + "_term", b, h, g)] = term
 
         def mix_values(b, h, g):
             if g == 0:
                 kept[("vm_grouped", b, h)] = entries.tile(
                     [P, PASSES, D, PACK], BF16, name="vm_grouped%d" % h, align_bytes=64
                 )
-            nc.vector.scalar_tensor_tensor(
-                out=kept[("vm_grouped", b, h)][:, g, :, :],
-                in0=kept[("v", b)][:, g * PACK : (g + 1) * PACK, h * D : (h + 1) * D].rearrange("p t d -> p d t"),
-                scalar=lam1[:, 0:1],
-                in1=kept[("second_term", b, h, g)][:],
-                op0=ALU.mult,
-                op1=ALU.add,
-            )
+            grouped = kept[("vm_grouped", b, h)][:, g, :, :]
+            second = kept[("v1_term", b, h, g)]
+            if b == 0:
+                nc.vector.scalar_tensor_tensor(
+                    out=grouped,
+                    in0=kept[("v", b)][:, g * PACK : (g + 1) * PACK, h * D : (h + 1) * D].rearrange("p t d -> p d t"),
+                    scalar=lam1[:, 0:1], in1=second[:], op0=ALU.mult, op1=ALU.add,
+                )
+            else:
+                scale_values("v", lam1, b, h, g)
+                first = kept[("v_term", b, h, g)]
+                for d in range(0, D, QUARTER):
+                    nc.gpsimd.tensor_tensor(
+                        out=grouped[:, d : d + QUARTER, :], in0=first[:, d : d + QUARTER, :],
+                        in1=second[:, d : d + QUARTER, :], op=ALU.add,
+                    )
 
         def quantise_values(b, h):
             codes = entries.tile([P, PASSES, D], U32, name="vm_codes%d" % h, align_bytes=64)
@@ -416,7 +424,7 @@ def tile_selfattention_pb_t_kernel(tc, q_rot, k_rot, v, v1, lamb1, lamb2, wproj,
                 for chunk in range(CHUNKS):
                     first_round, second_round = mixing_rounds(b, chunk)
                     if r == first_round:
-                        scale_second_values(b, *divmod(chunk, PASSES))
+                        scale_values("v1", lam2, b, *divmod(chunk, PASSES))
                     if r == second_round:
                         mix_values(b, *divmod(chunk, PASSES))
             h = r_in_entry - (PV_LAG - H)

@@ -33,18 +33,30 @@ QUADS = STEPS // QUAD
 
 FLIP_LAG = 3
 QUANT_LAG = 5
-SPREAD_LAG = 7
-PV_LAG = 8
-OUT_LAG = PV_LAG + 5
-ROUNDS = QUAD * (QUADS - 1) + OUT_LAG + 2
-W_ROUND = 1
+INVERT_LAG = 5
+PV_LAG = 12
+VALUES_LAG = 9
+LAST_PV_LAG = 8
+PV_GAP = 2
+OUT_GAP = 2
+BY_TENSOR = 2
+W_ROUND = 7
 
-FLIP_ORDER = (
-    ("k", 0, 0), ("k", 0, 1), ("q", 0, 0), ("k", 1, 0), ("k", 1, 1), ("q", 1, 0), ("q", 0, 1), ("q", 1, 1),
-)
-FLIP_UNITS = B * len(FLIP_ORDER)
-FLIPS_AHEAD = 6
-FLIP_PERIOD = STEPS_PER_ENTRY // len(FLIP_ORDER)
+FLIP_ORDER = (("q", 0), ("k", 0, 0), ("k", 0, 1), ("k", 1, 0), ("k", 1, 1), ("q", 1), ("q", 2), ("q", 3))
+UNITS = len(FLIP_ORDER)
+FLIPS_FIRST = 3
+FLIP_LEAD = 12
+FLIP_PERIOD = STEPS_PER_ENTRY // UNITS
+
+
+def units_of_round(r):
+    if r < 0:
+        return []
+    first = {0: [3, 4], 1: [5], 2: [6], 3: [7]}.get(r, [])
+    index, off_beat = divmod(r + FLIP_LEAD, FLIP_PERIOD)
+    later = [index] if off_beat == 0 and UNITS <= index < B * UNITS else []
+    return first + later
+
 
 CHUNKS = H * PASSES
 MIX_LEAD = 8
@@ -56,6 +68,24 @@ FLOPS = 2 * B * H * T * T * D * 2 + 2 * B * T * HD * C
 def due(r, lag, period, count):
     index, off_beat = divmod(r - lag, period)
     return index if off_beat == 0 and 0 <= index < count else None
+
+
+def attend_round(quad, i):
+    if i == 1 and quad == QUADS - 1:
+        return attend_round(quad, 0) + 1
+    return QUAD * quad + min(PV_LAG, LAST_PV_LAG + QUADS - 1 - quad) + PV_GAP * i
+
+
+RESULTS = [(quad, (0, 1)) for quad in range(QUADS - 1)] + [(QUADS - 1, (0,)), (QUADS - 1, (1,))]
+ROUNDS = attend_round(QUADS - 1, 1) + OUT_GAP + 2
+
+
+def attended_in(r):
+    return [(quad, i) for quad in range(QUADS) for i in range(2) if attend_round(quad, i) == r]
+
+
+def projected_in(r):
+    return [n for n, (quad, tiles) in enumerate(RESULTS) if attend_round(quad, tiles[-1]) + OUT_GAP == r]
 
 
 def place(step):
@@ -88,29 +118,43 @@ def tile_selfattention_pb_t_kernel(tc, q_rot, k_rot, v, v1, lamb1, lamb2, wproj,
         ident_f32 = const.tile([P, P], F32)
         make_identity(nc, ident_f32[:])
 
-        def load_tokens(name, source, b):
-            tokens = entries.tile([P, TILES, HD], BF16, name=name)
-            for g in range(PASSES):
-                nc.sync.dma_start(
-                    out=tokens[:, g * PACK : (g + 1) * PACK, :].rearrange("p t f -> p (t f)"),
-                    in_=source[b, g * K_PASS : (g + 1) * K_PASS].rearrange("(p t) h d -> p (t h d)", p=P),
-                )
-            kept[(name, b)] = tokens
+        SOURCES = (("k", k_rot), ("q", q_rot), ("v", v), ("v1", v1))
+        LOADS = len(SOURCES) * PASSES
 
-        def load_entry(b):
-            load_tokens("k", k_rot, b)
-            load_tokens("q", q_rot, b)
-            load_tokens("v", v, b)
-            load_tokens("v1", v1, b)
+        def load_piece(b, n):
+            name, source = SOURCES[n // PASSES]
+            g = n % PASSES
+            if g == 0:
+                kept[(name, b)] = entries.tile([P, TILES, HD], BF16, name=name)
+            nc.sync.dma_start(
+                out=kept[(name, b)][:, g * PACK : (g + 1) * PACK, :].rearrange("p t f -> p (t f)"),
+                in_=source[b, g * K_PASS : (g + 1) * K_PASS].rearrange("(p t) h d -> p (t h d)", p=P),
+            )
 
+        kept[("q", 0)] = entries.tile([P, TILES, HD], BF16, name="q")
+
+        def load_first_queries(first, last):
+            g, t = divmod(first, PACK)
+            nc.sync.dma_start(
+                out=kept[("q", 0)][:, first:last, :],
+                in_=q_rot[0, g * K_PASS : (g + 1) * K_PASS].rearrange("(p t) h d -> p t (h d)", t=PACK)[
+                    :, t : t + last - first, :
+                ],
+            )
+
+        load_first_queries(0, 2)
+        load_piece(0, 0)
+        load_piece(0, 1)
+        load_first_queries(2, 4)
+        load_first_queries(4, 8)
         lam1_bf = const.tile([P, 1], BF16)
         nc.sync.dma_start(out=lam1_bf[:], in_=lamb1.partition_broadcast(P))
         lam2_bf = const.tile([P, 1], BF16)
         nc.sync.dma_start(out=lam2_bf[:], in_=lamb2.partition_broadcast(P))
-        load_entry(0)
+        for n in range(2 * PASSES, LOADS):
+            load_piece(0, n)
         w_raw = const.tile([P, C // P, HD], BF16)
         nc.sync.dma_start(out=w_raw[:], in_=wproj.rearrange("(o p) k -> p o k", p=P))
-        load_entry(1)
         lam1 = const.tile([P, 1], F32)
         lam2 = const.tile([P, 1], F32)
 
@@ -174,9 +218,15 @@ def tile_selfattention_pb_t_kernel(tc, q_rot, k_rot, v, v1, lamb1, lamb2, wproj,
                 in_=w_grouped[:].rearrange("p c t -> p (c t)"),
             )
 
-        def transpose_half_head(unit):
-            b, k = divmod(unit, len(FLIP_ORDER))
-            name, h, half = FLIP_ORDER[k]
+        def transpose_unit(unit):
+            b, k = divmod(unit, UNITS)
+            name = FLIP_ORDER[k][0]
+            if name == "k":
+                h, half = FLIP_ORDER[k][1:]
+                pieces = [(h, half * PACK + t) for t in range(PACK)]
+            else:
+                j = FLIP_ORDER[k][1]
+                pieces = [(h, 2 * j + i) for h in range(H) for i in range(2)]
             words = (
                 kept[(name, b)][:]
                 .rearrange("p c f -> p (c f)")
@@ -184,38 +234,40 @@ def tile_selfattention_pb_t_kernel(tc, q_rot, k_rot, v, v1, lamb1, lamb2, wproj,
                 .rearrange("p (c w) -> p c w", c=TILES)
             )
             bank = psum_spare.tile([P, PACK, P], F32, name="spare_bank")
-            for j in range(PACK):
-                nc.tensor.transpose(
-                    bank[:, j, :], words[:, half * PACK + j, h * WORDS : (h + 1) * WORDS], ident_f32[:]
-                )
+            for n, (h, c) in enumerate(pieces):
+                nc.tensor.transpose(bank[:, n, :], words[:, c, h * WORDS : (h + 1) * WORDS], ident_f32[:])
             kept[("flip_bank", unit)] = bank
 
-        def copy_half_head(unit):
-            b, k = divmod(unit, len(FLIP_ORDER))
-            name, h, half = FLIP_ORDER[k]
+        def copy_unit(unit, copy):
+            b, k = divmod(unit, UNITS)
+            name = FLIP_ORDER[k][0]
             if (name + "_words", b) not in kept:
-                flipped = entries.tile([P, H, T], F32, name=name + "_flipped")
+                shape = [P, H, T] if name == "k" else [P, TILES // 2, H * 2 * P]
+                flipped = entries.tile(shape, F32, name=name + "_flipped")
                 kept[(name + "_words", b)] = flipped
                 kept[(name + "_pairs", b)] = (
-                    flipped[:].rearrange("p h n -> p (h n)").bitcast(BF16).rearrange("p (h n e) -> p h n e", h=H, e=2)
+                    flipped[:].rearrange("p x n -> p (x n)").bitcast(BF16).rearrange("p (x n e) -> p x n e", x=shape[1], e=2)
                 )
-            out = kept[(name + "_words", b)][:, h, half * BANK : (half + 1) * BANK]
+            flipped = kept[(name + "_words", b)]
             bank = kept[("flip_bank", unit)]
             if name == "k":
-                nc.scalar.copy(
-                    out=out.rearrange("p (u r e) -> p u r e", u=2, e=2),
+                h, half = FLIP_ORDER[k][1:]
+                copy(
+                    out=flipped[:, h, half * BANK : (half + 1) * BANK].rearrange("p (u r e) -> p u r e", u=2, e=2),
                     in_=bank[:].rearrange("p (u e) r -> p u r e", e=2),
                 )
             else:
-                nc.scalar.copy(out=out, in_=bank[:].rearrange("p j r -> p (j r)"))
+                j = FLIP_ORDER[k][1]
+                copy(out=flipped[:, j, :], in_=bank[:].rearrange("p n r -> p (n r)"))
 
         def score_matmul(step, half, parity):
             b, h, tile_index = place(step)
+            place_in_quad = 2 * h + tile_index % 2
             if parity == 0:
                 kept[("scores", step, half)] = psum_scores.tile([P, BANK], F32, name="score_bank")
             nc.tensor.matmul(
                 kept[("scores", step, half)][:],
-                lhsT=kept[("q_pairs", b)][:, h, tile_index * P : (tile_index + 1) * P, parity],
+                lhsT=kept[("q_pairs", b)][:, tile_index // 2, place_in_quad * P : (place_in_quad + 1) * P, parity],
                 rhs=kept[("k_pairs", b)][:, h, half * BANK : (half + 1) * BANK, parity],
                 start=(parity == 0),
                 stop=(parity == 1),
@@ -259,7 +311,8 @@ def tile_selfattention_pb_t_kernel(tc, q_rot, k_rot, v, v1, lamb1, lamb2, wproj,
 
         def group_probabilities(step):
             grouped = rounds.tile([P, PASSES, P, PACK], BF16, name="e_grouped", align_bytes=64)
-            nc.scalar.copy(
+            copy = nc.vector.tensor_copy if step == STEPS - 2 else nc.scalar.copy
+            copy(
                 out=grouped[:].bitcast(F32),
                 in_=kept[("e_flipped", step)][:].rearrange("p (g u) q -> p g q u", g=PASSES),
             )
@@ -277,25 +330,36 @@ def tile_selfattention_pb_t_kernel(tc, q_rot, k_rot, v, v1, lamb1, lamb2, wproj,
             )
 
         def invert_row_sums(quad):
-            inverse = rounds.tile([P, QUAD], F32, name="inverse")
-            nc.vector.reciprocal(out=inverse[:], in_=kept[("row_sums", quad)][:])
+            inverse = rounds.tile([P, 2, QUAD], F32, name="inverse")
+            nc.vector.reciprocal(
+                out=inverse[:], in_=kept[("row_sums", quad)][:].unsqueeze(1).to_broadcast([P, 2, QUAD])
+            )
             kept[("inverse", quad)] = inverse
 
-        def spread_row_sums(quad):
+        def spread_by_dma(quad):
+            rows = P * 2 * QUAD // C
+            first = T - K_PASS + rows * quad
+            borrowed = out[B - 1, first : first + rows, :].rearrange("r c -> (r c)")
+            nc.sync.dma_start(
+                out=borrowed.rearrange("(p s) -> p s", p=P),
+                in_=kept[("inverse", quad)][:].rearrange("p u s -> p (u s)"),
+            )
+            spread = rounds.tile([P, P, 2 * QUAD], F32, name="spread")
+            nc.sync.dma_start(out=spread[:].rearrange("p q s -> p (q s)"), in_=borrowed.partition_broadcast(P))
+            kept[("spread", quad)] = spread[:, :, 0:QUAD]
+
+        def spread_by_tensor(quad):
             bank = psum_spare.tile([P, QUAD, P], F32, name="spare_bank")
             for slot in range(QUAD):
                 nc.tensor.transpose(
-                    bank[:, slot, :], kept[("inverse", quad)][:, slot : slot + 1].to_broadcast([P, P]), ident_f32[:]
+                    bank[:, slot, :], kept[("inverse", quad)][:, 0, slot : slot + 1].to_broadcast([P, P]), ident_f32[:]
                 )
             kept[("spread_bank", quad)] = bank
 
         def copy_spread_row_sums(quad):
-            spread = rounds.tile([P, H, 2, P], F32, name="spread")
-            nc.vector.tensor_copy(
-                out=spread[:].rearrange("p h i q -> p (h i q)"),
-                in_=kept[("spread_bank", quad)][:].rearrange("p c q -> p (c q)"),
-            )
-            kept[("spread", quad)] = spread
+            spread = rounds.tile([P, QUAD, P], F32, name="spread_last")
+            nc.vector.tensor_copy(out=spread[:], in_=kept[("spread_bank", quad)][:])
+            kept[("spread", quad)] = spread[:].rearrange("p s q -> p q s")
 
         def attend(quad, i):
             b = place(QUAD * quad)[0]
@@ -320,66 +384,69 @@ def tile_selfattention_pb_t_kernel(tc, q_rot, k_rot, v, v1, lamb1, lamb2, wproj,
             nc.vector.tensor_tensor(
                 out=kept[("y_grouped", quad)][:, i, :, :].rearrange("p q (h e) -> p q h e", h=H),
                 in0=kept[("y_bank", quad, i)][:].rearrange("p (h e) q -> p q h e", h=H),
-                in1=kept[("spread", quad)][:, :, i, :].rearrange("p h q -> p q h").unsqueeze(3).to_broadcast([P, P, H, BLOCKS]),
+                in1=kept[("spread", quad)][:, :, i : QUAD : 2].unsqueeze(3).to_broadcast([P, P, H, BLOCKS]),
                 op=ALU.mult,
             )
 
-        def quantise_outputs(quad):
+        def quantise_outputs(n):
+            quad, tiles = RESULTS[n]
             codes = rounds.tile([P, 2, P], U32, name="y_codes", align_bytes=64)
             scales = rounds.tile([P, 2, P], U8, name="y_scales", align_bytes=64)
+            count = len(tiles)
             nc.vector.quantize_mx(
-                out=codes[:].rearrange("p i q -> p (i q)").bitcast(FP8X4),
-                scales=scales[:].rearrange("p i q -> p (i q)"),
-                in_=kept[("y_grouped", quad)][:].rearrange("p i q t -> p (i q t)"),
+                out=codes[:, :count, :].rearrange("p i q -> p (i q)").bitcast(FP8X4),
+                scales=scales[:, :count, :].rearrange("p i q -> p (i q)"),
+                in_=kept[("y_grouped", quad)][:, tiles[0] : tiles[0] + count, :, :].rearrange("p i q t -> p (i q t)"),
             )
-            kept[("y_codes", quad)] = codes
-            kept[("y_scales", quad)] = scales
+            kept[("y_codes", n)] = codes
+            kept[("y_scales", n)] = scales
 
-        def project(quad):
+        def project(n):
             bank = psum_spare.tile([P, 2, C], F32, name="spare_bank")
-            for i in range(2):
+            for i in range(len(RESULTS[n][1])):
                 nc.tensor.matmul_mx(
                     out=bank[:, i, :],
-                    lhsT=kept[("y_codes", quad)][:, i, :].bitcast(FP8X4),
-                    lhsT_scale=kept[("y_scales", quad)][:, i, :],
+                    lhsT=kept[("y_codes", n)][:, i, :].bitcast(FP8X4),
+                    lhsT_scale=kept[("y_scales", n)][:, i, :],
                     rhs=w_codes[:].bitcast(FP8X4),
                     rhs_scale=w_scales[:],
                     start=True,
                     stop=True,
                 )
-            kept[("out_bank", quad)] = bank
+            kept[("out_bank", n)] = bank
 
-        def store_result(quad):
+        def store_result(n):
+            quad, tiles = RESULTS[n]
             b, h, first_tile = place(QUAD * quad)
-            g, t_first = divmod(first_tile, PACK)
+            g, t_first = divmod(first_tile + tiles[0], PACK)
+            count = len(tiles)
             result = rounds.tile([P, 2, C], F32, name="result")
-            nc.scalar.copy(out=result[:], in_=kept[("out_bank", quad)][:])
+            nc.scalar.copy(out=result[:, :count, :], in_=kept[("out_bank", n)][:, :count, :])
             tokens_of_pass = out[b, g * K_PASS : (g + 1) * K_PASS, :].rearrange("(p t) c -> p t c", t=PACK)
-            nc.sync.dma_start(out=tokens_of_pass[:, t_first : t_first + 2, :], in_=result[:])
+            nc.sync.dma_start(out=tokens_of_pass[:, t_first : t_first + count, :], in_=result[:, :count, :])
 
-        for unit in range(FLIPS_AHEAD):
-            transpose_half_head(unit)
-            copy_half_head(unit)
-        nc.vector.tensor_copy(out=lam1[:], in_=lam1_bf[:])
-        nc.vector.tensor_copy(out=lam2[:], in_=lam2_bf[:])
+        for unit in range(FLIPS_FIRST):
+            transpose_unit(unit)
+            copy_unit(unit, nc.vector.tensor_copy if unit == 1 else nc.scalar.copy)
 
         for r in range(ROUNDS):
             entry_now, r_in_entry = divmod(r, STEPS_PER_ENTRY)
-            if r_in_entry == STEPS_PER_ENTRY // 2 and entry_now + 2 < B:
-                load_entry(entry_now + 2)
+            if r < LOADS:
+                load_piece(1, r)
+            piece = r_in_entry - STEPS_PER_ENTRY // 2
+            if entry_now + 2 < B and 0 <= piece < LOADS:
+                load_piece(entry_now + 2, piece)
 
-            late_unit = due(r - 1, 0, FLIP_PERIOD, FLIP_UNITS - FLIPS_AHEAD)
-            if late_unit is not None:
-                copy_half_head(FLIPS_AHEAD + late_unit)
-            quad = due(r - 1, SPREAD_LAG, QUAD, QUADS)
-            if quad is not None:
+            for n, unit in enumerate(units_of_round(r - 1)):
+                copy_unit(unit, nc.vector.tensor_copy if n else nc.scalar.copy)
+            quad = due(r - 1, INVERT_LAG, QUAD, QUADS)
+            if quad is not None and quad >= QUADS - BY_TENSOR:
                 copy_spread_row_sums(quad)
-            attended = due(r - 1, PV_LAG, 2, 2 * QUADS)
-            if attended is not None:
-                normalise(*divmod(attended, 2))
-            quad = due(r - 1, OUT_LAG, QUAD, QUADS)
-            if quad is not None:
-                store_result(quad)
+            attended = attended_in(r - 1)
+            for quad, i in attended:
+                normalise(quad, i)
+            for n in projected_in(r - 1):
+                store_result(n)
 
             flipping = 0 <= r - FLIP_LAG < STEPS
             for piece in range(2 * HALVES):
@@ -392,11 +459,14 @@ def tile_selfattention_pb_t_kernel(tc, q_rot, k_rot, v, v1, lamb1, lamb2, wproj,
                 scale_and_bound(r, 0)
             if 0 <= r - QUANT_LAG < STEPS:
                 quantise_probabilities(r - QUANT_LAG)
-            if attended is not None and attended % 2 == 1:
-                quantise_outputs(attended // 2)
-            quad = due(r, SPREAD_LAG - 1, QUAD, QUADS)
+            for n, (quad, tiles) in enumerate(RESULTS):
+                if (quad, tiles[-1]) in attended:
+                    quantise_outputs(n)
+            quad = due(r, INVERT_LAG, QUAD, QUADS)
             if quad is not None:
                 invert_row_sums(quad)
+                if quad < QUADS - BY_TENSOR:
+                    spread_by_dma(quad)
             if r < STEPS:
                 scale_and_bound(r, 1)
 
@@ -405,21 +475,21 @@ def tile_selfattention_pb_t_kernel(tc, q_rot, k_rot, v, v1, lamb1, lamb2, wproj,
             if r < STEPS:
                 exponentials(r)
 
-            late_unit = due(r, 0, FLIP_PERIOD, FLIP_UNITS - FLIPS_AHEAD)
-            if late_unit is not None:
-                transpose_half_head(FLIPS_AHEAD + late_unit)
+            for unit in units_of_round(r):
+                transpose_unit(unit)
             if r == W_ROUND:
                 prepare_weights()
-            quad = due(r, SPREAD_LAG, QUAD, QUADS)
-            if quad is not None:
-                spread_row_sums(quad)
-            attending = due(r, PV_LAG, 2, 2 * QUADS)
-            if attending is not None:
-                attend(*divmod(attending, 2))
-            quad = due(r, OUT_LAG, QUAD, QUADS)
-            if quad is not None:
-                project(quad)
+            quad = due(r, INVERT_LAG, QUAD, QUADS)
+            if quad is not None and quad >= QUADS - BY_TENSOR:
+                spread_by_tensor(quad)
+            for quad, i in attended_in(r):
+                attend(quad, i)
+            for n in projected_in(r):
+                project(n)
 
+            if r == 0:
+                nc.vector.tensor_copy(out=lam1[:], in_=lam1_bf[:])
+                nc.vector.tensor_copy(out=lam2[:], in_=lam2_bf[:])
             for b in range(B):
                 for chunk in range(CHUNKS):
                     first_round, second_round = mixing_rounds(b, chunk)
@@ -427,6 +497,6 @@ def tile_selfattention_pb_t_kernel(tc, q_rot, k_rot, v, v1, lamb1, lamb2, wproj,
                         scale_values("v1", lam2, b, *divmod(chunk, PASSES))
                     if r == second_round:
                         mix_values(b, *divmod(chunk, PASSES))
-            h = r_in_entry - (PV_LAG - H)
+            h = r_in_entry - VALUES_LAG
             if r < STEPS and 0 <= h < H:
                 quantise_values(entry_now, h)

@@ -35,12 +35,13 @@ FLIP_LAG = 3
 QUANT_LAG = 5
 INVERT_LAG = 5
 PV_LAG = 12
+FIRST_VALUES_LAG = 10
 VALUES_LAG = 9
 LAST_PV_LAG = 8
 PV_GAP = 2
-OUT_GAP = 2
+OUT_GAP = 3
 BY_TENSOR = 2
-W_ROUND = 7
+W_ROUND = 11
 
 FLIP_ORDER = (("q", 0), ("k", 0, 0), ("k", 0, 1), ("k", 1, 0), ("k", 1, 1), ("q", 1), ("q", 2), ("q", 3))
 UNITS = len(FLIP_ORDER)
@@ -96,7 +97,9 @@ def place(step):
 
 
 def mixing_rounds(b, chunk):
-    first = chunk if b == 0 else b * STEPS_PER_ENTRY - MIX_LEAD + QUAD * chunk
+    if b == 0:
+        return chunk, (3 + 2 * chunk if chunk < PASSES else chunk)
+    first = b * STEPS_PER_ENTRY - MIX_LEAD + QUAD * chunk
     return first, first + MIX_GAP
 
 
@@ -118,40 +121,46 @@ def tile_selfattention_pb_t_kernel(tc, q_rot, k_rot, v, v1, lamb1, lamb2, wproj,
         ident_f32 = const.tile([P, P], F32)
         make_identity(nc, ident_f32[:])
 
-        SOURCES = (("k", k_rot), ("q", q_rot), ("v", v), ("v1", v1))
-        LOADS = len(SOURCES) * PASSES
-
-        def load_piece(b, n):
-            name, source = SOURCES[n // PASSES]
-            g = n % PASSES
-            if g == 0:
-                kept[(name, b)] = entries.tile([P, TILES, HD], BF16, name=name)
+        def load_keys(b, h, g):
+            if (h, g) == (0, 0):
+                kept[("k", b)] = entries.tile([P, H, TILES, D], BF16, name="k")
             nc.sync.dma_start(
-                out=kept[(name, b)][:, g * PACK : (g + 1) * PACK, :].rearrange("p t f -> p (t f)"),
-                in_=source[b, g * K_PASS : (g + 1) * K_PASS].rearrange("(p t) h d -> p (t h d)", p=P),
+                out=kept[("k", b)][:, h, g * PACK : (g + 1) * PACK, :],
+                in_=k_rot[b, g * K_PASS : (g + 1) * K_PASS, h].rearrange("(p t) d -> p t d", t=PACK),
             )
 
-        kept[("q", 0)] = entries.tile([P, TILES, HD], BF16, name="q")
-
-        def load_first_queries(first, last):
+        def load_tokens(name, source, b, first, last):
+            if first == 0:
+                kept[(name, b)] = entries.tile([P, TILES, HD], BF16, name=name)
             g, t = divmod(first, PACK)
             nc.sync.dma_start(
-                out=kept[("q", 0)][:, first:last, :],
-                in_=q_rot[0, g * K_PASS : (g + 1) * K_PASS].rearrange("(p t) h d -> p t (h d)", t=PACK)[
+                out=kept[(name, b)][:, first:last, :],
+                in_=source[b, g * K_PASS : (g + 1) * K_PASS].rearrange("(p t) h d -> p t (h d)", t=PACK)[
                     :, t : t + last - first, :
                 ],
             )
 
-        load_first_queries(0, 2)
+        def load_piece(b, n):
+            if n < H:
+                for g in range(PASSES):
+                    load_keys(b, n, g)
+            else:
+                name, source = (("q", q_rot), ("v", v), ("v1", v1))[(n - H) // PASSES]
+                g = (n - H) % PASSES
+                load_tokens(name, source, b, g * PACK, (g + 1) * PACK)
+
+        LOADS = H + 3 * PASSES
+
+        load_tokens("q", q_rot, 0, 0, 2)
         load_piece(0, 0)
         load_piece(0, 1)
-        load_first_queries(2, 4)
-        load_first_queries(4, 8)
+        load_tokens("q", q_rot, 0, 2, PACK)
+        load_tokens("q", q_rot, 0, PACK, TILES)
         lam1_bf = const.tile([P, 1], BF16)
         nc.sync.dma_start(out=lam1_bf[:], in_=lamb1.partition_broadcast(P))
         lam2_bf = const.tile([P, 1], BF16)
         nc.sync.dma_start(out=lam2_bf[:], in_=lamb2.partition_broadcast(P))
-        for n in range(2 * PASSES, LOADS):
+        for n in range(H + PASSES, LOADS):
             load_piece(0, n)
         w_raw = const.tile([P, C // P, HD], BF16)
         nc.sync.dma_start(out=w_raw[:], in_=wproj.rearrange("(o p) k -> p o k", p=P))
@@ -175,7 +184,7 @@ def tile_selfattention_pb_t_kernel(tc, q_rot, k_rot, v, v1, lamb1, lamb2, wproj,
                 )
             grouped = kept[("vm_grouped", b, h)][:, g, :, :]
             second = kept[("v1_term", b, h, g)]
-            if b == 0:
+            if b == 0 and h == 0:
                 nc.vector.scalar_tensor_tensor(
                     out=grouped,
                     in0=kept[("v", b)][:, g * PACK : (g + 1) * PACK, h * D : (h + 1) * D].rearrange("p t d -> p d t"),
@@ -227,15 +236,11 @@ def tile_selfattention_pb_t_kernel(tc, q_rot, k_rot, v, v1, lamb1, lamb2, wproj,
             else:
                 j = FLIP_ORDER[k][1]
                 pieces = [(h, 2 * j + i) for h in range(H) for i in range(2)]
-            words = (
-                kept[(name, b)][:]
-                .rearrange("p c f -> p (c f)")
-                .bitcast(F32)
-                .rearrange("p (c w) -> p c w", c=TILES)
-            )
+            tokens = kept[(name, b)][:]
             bank = psum_spare.tile([P, PACK, P], F32, name="spare_bank")
             for n, (h, c) in enumerate(pieces):
-                nc.tensor.transpose(bank[:, n, :], words[:, c, h * WORDS : (h + 1) * WORDS], ident_f32[:])
+                features = tokens[:, h, c, :] if name == "k" else tokens[:, c, h * D : (h + 1) * D]
+                nc.tensor.transpose(bank[:, n, :], features.bitcast(F32), ident_f32[:])
             kept[("flip_bank", unit)] = bank
 
         def copy_unit(unit, copy):
@@ -311,8 +316,7 @@ def tile_selfattention_pb_t_kernel(tc, q_rot, k_rot, v, v1, lamb1, lamb2, wproj,
 
         def group_probabilities(step):
             grouped = rounds.tile([P, PASSES, P, PACK], BF16, name="e_grouped", align_bytes=64)
-            copy = nc.vector.tensor_copy if step == STEPS - 2 else nc.scalar.copy
-            copy(
+            nc.scalar.copy(
                 out=grouped[:].bitcast(F32),
                 in_=kept[("e_flipped", step)][:].rearrange("p (g u) q -> p g q u", g=PASSES),
             )
@@ -420,7 +424,7 @@ def tile_selfattention_pb_t_kernel(tc, q_rot, k_rot, v, v1, lamb1, lamb2, wproj,
             b, h, first_tile = place(QUAD * quad)
             g, t_first = divmod(first_tile + tiles[0], PACK)
             count = len(tiles)
-            result = rounds.tile([P, 2, C], F32, name="result")
+            result = rounds.tile([P, 2, C], F32, name="result", bufs=5)
             nc.scalar.copy(out=result[:, :count, :], in_=kept[("out_bank", n)][:, :count, :])
             tokens_of_pass = out[b, g * K_PASS : (g + 1) * K_PASS, :].rearrange("(p t) c -> p t c", t=PACK)
             nc.sync.dma_start(out=tokens_of_pass[:, t_first : t_first + count, :], in_=result[:, :count, :])
@@ -479,13 +483,13 @@ def tile_selfattention_pb_t_kernel(tc, q_rot, k_rot, v, v1, lamb1, lamb2, wproj,
                 transpose_unit(unit)
             if r == W_ROUND:
                 prepare_weights()
-            quad = due(r, INVERT_LAG, QUAD, QUADS)
-            if quad is not None and quad >= QUADS - BY_TENSOR:
-                spread_by_tensor(quad)
             for quad, i in attended_in(r):
                 attend(quad, i)
             for n in projected_in(r):
                 project(n)
+            quad = due(r, INVERT_LAG, QUAD, QUADS)
+            if quad is not None and quad >= QUADS - BY_TENSOR:
+                spread_by_tensor(quad)
 
             if r == 0:
                 nc.vector.tensor_copy(out=lam1[:], in_=lam1_bf[:])
@@ -497,6 +501,6 @@ def tile_selfattention_pb_t_kernel(tc, q_rot, k_rot, v, v1, lamb1, lamb2, wproj,
                         scale_values("v1", lam2, b, *divmod(chunk, PASSES))
                     if r == second_round:
                         mix_values(b, *divmod(chunk, PASSES))
-            h = r_in_entry - VALUES_LAG
+            h = r_in_entry - (FIRST_VALUES_LAG if entry_now == 0 else VALUES_LAG)
             if r < STEPS and 0 <= h < H:
                 quantise_values(entry_now, h)

@@ -23,7 +23,7 @@ BANK = 512
 HALVES = T // BANK
 WORDS = D // 2
 BLOCKS = D // P
-QUARTER = D // 4
+QUARTER = D // 2
 SCALE = 1.0 / 16.0
 
 QUAD = 2 * H
@@ -33,6 +33,7 @@ QUADS = STEPS // QUAD
 
 FLIP_LAG = 3
 QUANT_LAG = 5
+FIRST_QUANT_LAG = 6
 INVERT_LAG = 5
 PV_LAG = 12
 FIRST_VALUES_LAG = 10
@@ -79,6 +80,10 @@ def attend_round(quad, i):
 
 RESULTS = [(quad, (0, 1)) for quad in range(QUADS - 1)] + [(QUADS - 1, (0,)), (QUADS - 1, (1,))]
 ROUNDS = attend_round(QUADS - 1, 1) + OUT_GAP + 2
+
+
+def quantised_in(r):
+    return [s for s in range(STEPS) if s + (FIRST_QUANT_LAG if s < STEPS_PER_ENTRY else QUANT_LAG) == r]
 
 
 def attended_in(r):
@@ -334,36 +339,42 @@ def tile_selfattention_pb_t_kernel(tc, q_rot, k_rot, v, v1, lamb1, lamb2, wproj,
             )
 
         def invert_row_sums(quad):
-            inverse = rounds.tile([P, 2, QUAD], F32, name="inverse")
+            inverse = rounds.tile([P, 2, H, BLOCKS], F32, name="inverse")
             nc.vector.reciprocal(
-                out=inverse[:], in_=kept[("row_sums", quad)][:].unsqueeze(1).to_broadcast([P, 2, QUAD])
+                out=inverse[:],
+                in_=kept[("row_sums", quad)][:].rearrange("p (h i) -> p i h", h=H).unsqueeze(3).to_broadcast([P, 2, H, BLOCKS]),
             )
             kept[("inverse", quad)] = inverse
 
         def spread_by_dma(quad):
-            rows = P * 2 * QUAD // C
+            rows = P * 2 * PACK // C
             first = T - K_PASS + rows * quad
             borrowed = out[B - 1, first : first + rows, :].rearrange("r c -> (r c)")
             nc.sync.dma_start(
                 out=borrowed.rearrange("(p s) -> p s", p=P),
-                in_=kept[("inverse", quad)][:].rearrange("p u s -> p (u s)"),
+                in_=kept[("inverse", quad)][:].rearrange("p i h e -> p (i h e)"),
             )
-            spread = rounds.tile([P, P, 2 * QUAD], F32, name="spread")
-            nc.sync.dma_start(out=spread[:].rearrange("p q s -> p (q s)"), in_=borrowed.partition_broadcast(P))
-            kept[("spread", quad)] = spread[:, :, 0:QUAD]
+            spread = rounds.tile([P, P, 2, PACK], F32, name="spread", align_bytes=64)
+            nc.sync.dma_start(out=spread[:].rearrange("p q i t -> p (q i t)"), in_=borrowed.partition_broadcast(P))
+            for i in range(2):
+                kept[("spread", quad, i)] = spread[:, :, i, :].rearrange("p q (h e) -> p q h e", h=H)
 
         def spread_by_tensor(quad):
             bank = psum_spare.tile([P, QUAD, P], F32, name="spare_bank")
             for slot in range(QUAD):
+                h, i = divmod(slot, 2)
                 nc.tensor.transpose(
-                    bank[:, slot, :], kept[("inverse", quad)][:, 0, slot : slot + 1].to_broadcast([P, P]), ident_f32[:]
+                    bank[:, slot, :], kept[("inverse", quad)][:, i, h, 0:1].to_broadcast([P, P]), ident_f32[:]
                 )
             kept[("spread_bank", quad)] = bank
 
         def copy_spread_row_sums(quad):
             spread = rounds.tile([P, QUAD, P], F32, name="spread_last")
-            nc.vector.tensor_copy(out=spread[:], in_=kept[("spread_bank", quad)][:])
-            kept[("spread", quad)] = spread[:].rearrange("p s q -> p q s")
+            nc.scalar.copy(out=spread[:], in_=kept[("spread_bank", quad)][:])
+            for i in range(2):
+                kept[("spread", quad, i)] = (
+                    spread[:, i:QUAD:2, :].rearrange("p h q -> p q h").unsqueeze(3).to_broadcast([P, P, H, BLOCKS])
+                )
 
         def attend(quad, i):
             b = place(QUAD * quad)[0]
@@ -388,7 +399,7 @@ def tile_selfattention_pb_t_kernel(tc, q_rot, k_rot, v, v1, lamb1, lamb2, wproj,
             nc.vector.tensor_tensor(
                 out=kept[("y_grouped", quad)][:, i, :, :].rearrange("p q (h e) -> p q h e", h=H),
                 in0=kept[("y_bank", quad, i)][:].rearrange("p (h e) q -> p q h e", h=H),
-                in1=kept[("spread", quad)][:, :, i : QUAD : 2].unsqueeze(3).to_broadcast([P, P, H, BLOCKS]),
+                in1=kept[("spread", quad, i)],
                 op=ALU.mult,
             )
 
@@ -442,7 +453,7 @@ def tile_selfattention_pb_t_kernel(tc, q_rot, k_rot, v, v1, lamb1, lamb2, wproj,
                 load_piece(entry_now + 2, piece)
 
             for n, unit in enumerate(units_of_round(r - 1)):
-                copy_unit(unit, nc.vector.tensor_copy if n else nc.scalar.copy)
+                copy_unit(unit, nc.scalar.copy)
             quad = due(r - 1, INVERT_LAG, QUAD, QUADS)
             if quad is not None and quad >= QUADS - BY_TENSOR:
                 copy_spread_row_sums(quad)
@@ -461,8 +472,8 @@ def tile_selfattention_pb_t_kernel(tc, q_rot, k_rot, v, v1, lamb1, lamb2, wproj,
 
             if r < STEPS:
                 scale_and_bound(r, 0)
-            if 0 <= r - QUANT_LAG < STEPS:
-                quantise_probabilities(r - QUANT_LAG)
+            for step in quantised_in(r):
+                quantise_probabilities(step)
             for n, (quad, tiles) in enumerate(RESULTS):
                 if (quad, tiles[-1]) in attended:
                     quantise_outputs(n)

from contextlib import ExitStack

import concourse.mybir as mybir
from concourse.masks import make_identity

F32 = mybir.dt.float32
BF16 = mybir.dt.bfloat16
U32 = mybir.dt.uint32
U8 = mybir.dt.uint8
FP8X4 = mybir.dt.float8_e4m3fn_x4
ALU = mybir.AluOpType
ACT = mybir.ActivationFunctionType

B, T, H, D = 4, 1024, 2, 256
HD = H * D
C = 256
P = 128
PACK = 4
K_PASS = P * PACK
PASSES = T // K_PASS
TILES = T // P
BANK = 512
HALVES = T // BANK
WORDS = D // 2
BLOCKS = D // P
QUARTER = D // 2
SCALE = 1.0 / 16.0

QUAD = 2 * H
STEPS_PER_ENTRY = H * TILES
STEPS = B * STEPS_PER_ENTRY
QUADS = STEPS // QUAD

FLIP_LAG = 3
QUANT_LAG = 5
FIRST_QUANT_LAG = 6
INVERT_LAG = 5
PV_LAG = 12
FIRST_VALUES_LAG = 10
VALUES_LAG = 9
LAST_PV_LAG = 8
PV_GAP = 2
OUT_GAP = 3
BY_TENSOR = 2
W_ROUND = 11

FLIP_ORDER = (("q", 0), ("k", 0, 0), ("k", 0, 1), ("k", 1, 0), ("k", 1, 1), ("q", 1), ("q", 2), ("q", 3))
UNITS = len(FLIP_ORDER)
FLIPS_FIRST = 3
FLIP_LEAD = 12
FLIP_PERIOD = STEPS_PER_ENTRY // UNITS


def units_of_round(r):
    if r < 0:
        return []
    first = {0: [3, 4], 1: [5], 2: [6], 3: [7]}.get(r, [])
    index, off_beat = divmod(r + FLIP_LEAD, FLIP_PERIOD)
    later = [index] if off_beat == 0 and UNITS <= index < B * UNITS else []
    return first + later


CHUNKS = H * PASSES
MIX_LEAD = 8
MIX_GAP = 2

FLOPS = 2 * B * H * T * T * D * 2 + 2 * B * T * HD * C


def due(r, lag, period, count):
    index, off_beat = divmod(r - lag, period)
    return index if off_beat == 0 and 0 <= index < count else None


def attend_round(quad, i):
    if i == 1 and quad == QUADS - 1:
        return attend_round(quad, 0) + 1
    return QUAD * quad + min(PV_LAG, LAST_PV_LAG + QUADS - 1 - quad) + PV_GAP * i


RESULTS = [(quad, (0, 1)) for quad in range(QUADS - 1)] + [(QUADS - 1, (0,)), (QUADS - 1, (1,))]
ROUNDS = attend_round(QUADS - 1, 1) + OUT_GAP + 2


def quantised_in(r):
    return [s for s in range(STEPS) if s + (FIRST_QUANT_LAG if s < STEPS_PER_ENTRY else QUANT_LAG) == r]


def attended_in(r):
    return [(quad, i) for quad in range(QUADS) for i in range(2) if attend_round(quad, i) == r]


def projected_in(r):
    return [n for n, (quad, tiles) in enumerate(RESULTS) if attend_round(quad, tiles[-1]) + OUT_GAP == r]


def place(step):
    b, rest = divmod(step, STEPS_PER_ENTRY)
    j, rest = divmod(rest, QUAD)
    h, i = divmod(rest, 2)
    return b, h, 2 * j + i


def mixing_rounds(b, chunk):
    if b == 0:
        return chunk, (3 + 2 * chunk if chunk < PASSES else chunk)
    first = b * STEPS_PER_ENTRY - MIX_LEAD + QUAD * chunk
    return first, first + MIX_GAP


def tile_selfattention_pb_t_kernel(tc, q_rot, k_rot, v, v1, lamb1, lamb2, wproj, out):
    nc = tc.nc
    with ExitStack() as ctx:
        const = ctx.enter_context(tc.tile_pool(name="const", bufs=1))
        entries = ctx.enter_context(tc.tile_pool(name="entries", bufs=2))
        rounds = ctx.enter_context(tc.tile_pool(name="rounds", bufs=3))
        psum_scores = ctx.enter_context(tc.psum_pool(name="psum_scores", bufs=3))
        psum_flips = ctx.enter_context(tc.psum_pool(name="psum_flips", bufs=2))
        psum_spare = ctx.enter_context(tc.psum_pool(name="psum_spare", bufs=3))
        ctx.enter_context(tc.manual_schedule())

        kept = {}

        ident_bf = const.tile([P, P], BF16)
        make_identity(nc, ident_bf[:])
        ident_f32 = const.tile([P, P], F32)
        make_identity(nc, ident_f32[:])

        def load_keys(b, h, g):
            if (h, g) == (0, 0):
                kept[("k", b)] = entries.tile([P, H, TILES, D], BF16, name="k")
            nc.sync.dma_start(
                out=kept[("k", b)][:, h, g * PACK : (g + 1) * PACK, :],
                in_=k_rot[b, g * K_PASS : (g + 1) * K_PASS, h].rearrange("(p t) d -> p t d", t=PACK),
            )

        def load_tokens(name, source, b, first, last):
            if first == 0:
                kept[(name, b)] = entries.tile([P, TILES, HD], BF16, name=name)
            g, t = divmod(first, PACK)
            nc.sync.dma_start(
                out=kept[(name, b)][:, first:last, :],
                in_=source[b, g * K_PASS : (g + 1) * K_PASS].rearrange("(p t) h d -> p t (h d)", t=PACK)[
                    :, t : t + last - first, :
                ],
            )

        def load_piece(b, n):
            if n < H:
                for g in range(PASSES):
                    load_keys(b, n, g)
            else:
                name, source = (("q", q_rot), ("v", v), ("v1", v1))[(n - H) // PASSES]
                g = (n - H) % PASSES
                load_tokens(name, source, b, g * PACK, (g + 1) * PACK)

        LOADS = H + 3 * PASSES

        load_tokens("q", q_rot, 0, 0, 2)
        load_piece(0, 0)
        load_piece(0, 1)
        load_tokens("q", q_rot, 0, 2, PACK)
        load_tokens("q", q_rot, 0, PACK, TILES)
        lam1_bf = const.tile([P, 1], BF16)
        nc.sync.dma_start(out=lam1_bf[:], in_=lamb1.partition_broadcast(P))
        lam2_bf = const.tile([P, 1], BF16)
        nc.sync.dma_start(out=lam2_bf[:], in_=lamb2.partition_broadcast(P))
        for n in range(H + PASSES, LOADS):
            load_piece(0, n)
        w_raw = const.tile([P, C // P, HD], BF16)
        nc.sync.dma_start(out=w_raw[:], in_=wproj.rearrange("(o p) k -> p o k", p=P))
        lam1 = const.tile([P, 1], F32)
        lam2 = const.tile([P, 1], F32)

        def scale_values(name, factor, b, h, g):
            term = rounds.tile([P, D, PACK], F32, name=name + "_term")
            source = kept[(name, b)][:, g * PACK : (g + 1) * PACK, h * D : (h + 1) * D].rearrange("p t d -> p d t")
            for d in range(0, D, QUARTER):
                nc.gpsimd.tensor_scalar(
                    out=term[:, d : d + QUARTER, :], in0=source[:, d : d + QUARTER, :],
                    scalar1=factor[:, 0:1], scalar2=0.0, op0=ALU.mult, op1=ALU.add,
                )
            kept[(name + "_term", b, h, g)] = term

        def mix_values(b, h, g):
            if g == 0:
                kept[("vm_grouped", b, h)] = entries.tile(
                    [P, PASSES, D, PACK], BF16, name="vm_grouped%d" % h, align_bytes=64
                )
            grouped = kept[("vm_grouped", b, h)][:, g, :, :]
            second = kept[("v1_term", b, h, g)]
            if b == 0 and h == 0:
                nc.vector.scalar_tensor_tensor(
                    out=grouped,
                    in0=kept[("v", b)][:, g * PACK : (g + 1) * PACK, h * D : (h + 1) * D].rearrange("p t d -> p d t"),
                    scalar=lam1[:, 0:1], in1=second[:], op0=ALU.mult, op1=ALU.add,
                )
            else:
                scale_values("v", lam1, b, h, g)
                first = kept[("v_term", b, h, g)]
                for d in range(0, D, QUARTER):
                    nc.gpsimd.tensor_tensor(
                        out=grouped[:, d : d + QUARTER, :], in0=first[:, d : d + QUARTER, :],
                        in1=second[:, d : d + QUARTER, :], op=ALU.add,
                    )

        def quantise_values(b, h):
            codes = entries.tile([P, PASSES, D], U32, name="vm_codes%d" % h, align_bytes=64)
            scales = entries.tile([P, PASSES, D], U8, name="vm_scales%d" % h, align_bytes=64)
            nc.vector.quantize_mx(
                out=codes[:].rearrange("p g d -> p (g d)").bitcast(FP8X4),
                scales=scales[:].rearrange("p g d -> p (g d)"),
                in_=kept[("vm_grouped", b, h)][:].rearrange("p g d t -> p (g d t)"),
            )
            kept[("vm_codes", b, h)] = codes
            kept[("vm_scales", b, h)] = scales

        w_codes = const.tile([P, C], U32, align_bytes=64)
        w_scales = const.tile([P, C], U8, align_bytes=64)

        def prepare_weights():
            w_flipped = psum_spare.tile([P, PACK, C], BF16, name="spare_bank")
            for o in range(C // P):
                for t in range(PACK):
                    nc.tensor.transpose(
                        w_flipped[:, t, o * P : (o + 1) * P], w_raw[:, o, t * P : (t + 1) * P], ident_bf[:]
                    )
            w_grouped = const.tile([P, C, PACK], BF16, align_bytes=64)
            nc.vector.tensor_copy(out=w_grouped[:], in_=w_flipped[:].rearrange("p t c -> p c t"))
            nc.vector.quantize_mx(
                out=w_codes[:].bitcast(FP8X4), scales=w_scales[:],
                in_=w_grouped[:].rearrange("p c t -> p (c t)"),
            )

        def transpose_unit(unit):
            b, k = divmod(unit, UNITS)
            name = FLIP_ORDER[k][0]
            if name == "k":
                h, half = FLIP_ORDER[k][1:]
                pieces = [(h, half * PACK + t) for t in range(PACK)]
            else:
                j = FLIP_ORDER[k][1]
                pieces = [(h, 2 * j + i) for h in range(H) for i in range(2)]
            tokens = kept[(name, b)][:]
            bank = psum_spare.tile([P, PACK, P], F32, name="spare_bank")
            for n, (h, c) in enumerate(pieces):
                features = tokens[:, h, c, :] if name == "k" else tokens[:, c, h * D : (h + 1) * D]
                nc.tensor.transpose(bank[:, n, :], features.bitcast(F32), ident_f32[:])
            kept[("flip_bank", unit)] = bank

        def copy_unit(unit, copy):
            b, k = divmod(unit, UNITS)
            name = FLIP_ORDER[k][0]
            if (name + "_words", b) not in kept:
                shape = [P, H, T] if name == "k" else [P, TILES // 2, H * 2 * P]
                flipped = entries.tile(shape, F32, name=name + "_flipped")
                kept[(name + "_words", b)] = flipped
                kept[(name + "_pairs", b)] = (
                    flipped[:].rearrange("p x n -> p (x n)").bitcast(BF16).rearrange("p (x n e) -> p x n e", x=shape[1], e=2)
                )
            flipped = kept[(name + "_words", b)]
            bank = kept[("flip_bank", unit)]
            if name == "k":
                h, half = FLIP_ORDER[k][1:]
                copy(
                    out=flipped[:, h, half * BANK : (half + 1) * BANK].rearrange("p (u r e) -> p u r e", u=2, e=2),
                    in_=bank[:].rearrange("p (u e) r -> p u r e", e=2),
                )
            else:
                j = FLIP_ORDER[k][1]
                copy(out=flipped[:, j, :], in_=bank[:].rearrange("p n r -> p (n r)"))

        def score_matmul(step, half, parity):
            b, h, tile_index = place(step)
            place_in_quad = 2 * h + tile_index % 2
            if parity == 0:
                kept[("scores", step, half)] = psum_scores.tile([P, BANK], F32, name="score_bank")
            nc.tensor.matmul(
                kept[("scores", step, half)][:],
                lhsT=kept[("q_pairs", b)][:, tile_index // 2, place_in_quad * P : (place_in_quad + 1) * P, parity],
                rhs=kept[("k_pairs", b)][:, h, half * BANK : (half + 1) * BANK, parity],
                start=(parity == 0),
                stop=(parity == 1),
            )

        def scale_and_bound(step, half):
            if half == 0:
                kept[("negated", step)] = rounds.tile([P, T], F32, name="negated")
                kept[("first_min", step)] = rounds.tile([P, 1], F32, name="first_min")
                kept[("bias", step)] = rounds.tile([P, 1], F32, name="bias")
            nc.vector.tensor_scalar(
                out=kept[("negated", step)][:, half * BANK : (half + 1) * BANK],
                in0=kept[("scores", step, half)][:],
                scalar1=-SCALE,
                scalar2=(None if half == 0 else kept[("first_min", step)][:, 0:1]),
                op0=ALU.mult,
                op1=ALU.min,
                accum_out=(kept[("first_min", step)][:] if half == 0 else kept[("bias", step)][:]),
            )

        def exponentials(step):
            quad, slot = divmod(step, QUAD)
            if slot == 0:
                kept[("row_sums", quad)] = rounds.tile([P, QUAD], F32, name="row_sums")
            e_rows = rounds.tile([P, T], BF16, name="e_rows", bufs=FLIP_LAG + 1)
            nc.scalar.activation(
                out=e_rows[:], in_=kept[("negated", step)][:], func=ACT.Exp,
                bias=kept[("bias", step)][:, 0:1], scale=-1.0,
                accum_out=kept[("row_sums", quad)][:, slot : slot + 1],
            )
            kept[("e_rows", step)] = e_rows

        def transpose_probabilities(step, c):
            if c == 0:
                kept[("e_flipped", step)] = psum_flips.tile([P, 2 * PASSES, P], F32, name="e_flipped")
            nc.tensor.transpose(
                kept[("e_flipped", step)][:, c, :],
                kept[("e_rows", step)][:].bitcast(F32)[:, c * P : (c + 1) * P],
                ident_f32[:],
            )

        def group_probabilities(step):
            grouped = rounds.tile([P, PASSES, P, PACK], BF16, name="e_grouped", align_bytes=64)
            nc.scalar.copy(
                out=grouped[:].bitcast(F32),
                in_=kept[("e_flipped", step)][:].rearrange("p (g u) q -> p g q u", g=PASSES),
            )
            kept[("e_grouped", step)] = grouped

        def quantise_probabilities(step):
            quad, slot = divmod(step, QUAD)
            if slot == 0:
                kept[("e_codes", quad)] = rounds.tile([P, QUAD, PASSES, P], U32, name="e_codes", align_bytes=64)
                kept[("e_scales", quad)] = rounds.tile([P, QUAD, PASSES, P], U8, name="e_scales", align_bytes=64)
            nc.vector.quantize_mx(
                out=kept[("e_codes", quad)][:, slot, :, :].rearrange("p g q -> p (g q)").bitcast(FP8X4),
                scales=kept[("e_scales", quad)][:, slot, :, :].rearrange("p g q -> p (g q)"),
                in_=kept[("e_grouped", step)][:].rearrange("p g q t -> p (g q t)"),
            )

        def invert_row_sums(quad):
            inverse = rounds.tile([P, 2, H, BLOCKS], F32, name="inverse")
            nc.vector.reciprocal(
                out=inverse[:],
                in_=kept[("row_sums", quad)][:].rearrange("p (h i) -> p i h", h=H).unsqueeze(3).to_broadcast([P, 2, H, BLOCKS]),
            )
            kept[("inverse", quad)] = inverse

        def spread_by_dma(quad):
            rows = P * 2 * PACK // C
            first = T - K_PASS + rows * quad
            borrowed = out[B - 1, first : first + rows, :].rearrange("r c -> (r c)")
            nc.sync.dma_start(
                out=borrowed.rearrange("(p s) -> p s", p=P),
                in_=kept[("inverse", quad)][:].rearrange("p i h e -> p (i h e)"),
            )
            spread = rounds.tile([P, P, 2, PACK], F32, name="spread", align_bytes=64)
            nc.sync.dma_start(out=spread[:].rearrange("p q i t -> p (q i t)"), in_=borrowed.partition_broadcast(P))
            for i in range(2):
                kept[("spread", quad, i)] = spread[:, :, i, :].rearrange("p q (h e) -> p q h e", h=H)

        def spread_by_tensor(quad):
            bank = psum_spare.tile([P, QUAD, P], F32, name="spare_bank")
            for slot in range(QUAD):
                h, i = divmod(slot, 2)
                nc.tensor.transpose(
                    bank[:, slot, :], kept[("inverse", quad)][:, i, h, 0:1].to_broadcast([P, P]), ident_f32[:]
                )
            kept[("spread_bank", quad)] = bank

        def copy_spread_row_sums(quad):
            spread = rounds.tile([P, QUAD, P], F32, name="spread_last")
            nc.scalar.copy(out=spread[:], in_=kept[("spread_bank", quad)][:])
            for i in range(2):
                kept[("spread", quad, i)] = (
                    spread[:, i:QUAD:2, :].rearrange("p h q -> p q h").unsqueeze(3).to_broadcast([P, P, H, BLOCKS])
                )

        def attend(quad, i):
            b = place(QUAD * quad)[0]
            bank = psum_spare.tile([P, PACK, P], F32, name="spare_bank")
            for t in range(PACK):
                h, block = divmod(t, BLOCKS)
                for g in range(PASSES):
                    nc.tensor.matmul_mx(
                        out=bank[:, t, :],
                        lhsT=kept[("vm_codes", b, h)][:, g, block * P : (block + 1) * P].bitcast(FP8X4),
                        lhsT_scale=kept[("vm_scales", b, h)][:, g, block * P : (block + 1) * P],
                        rhs=kept[("e_codes", quad)][:, 2 * h + i, g, :].bitcast(FP8X4),
                        rhs_scale=kept[("e_scales", quad)][:, 2 * h + i, g, :],
                        start=(g == 0),
                        stop=(g == PASSES - 1),
                    )
            kept[("y_bank", quad, i)] = bank

        def normalise(quad, i):
            if i == 0:
                kept[("y_grouped", quad)] = rounds.tile([P, 2, P, PACK], BF16, name="y_grouped", align_bytes=64)
            nc.vector.tensor_tensor(
                out=kept[("y_grouped", quad)][:, i, :, :].rearrange("p q (h e) -> p q h e", h=H),
                in0=kept[("y_bank", quad, i)][:].rearrange("p (h e) q -> p q h e", h=H),
                in1=kept[("spread", quad, i)],
                op=ALU.mult,
            )

        def quantise_outputs(n):
            quad, tiles = RESULTS[n]
            codes = rounds.tile([P, 2, P], U32, name="y_codes", align_bytes=64)
            scales = rounds.tile([P, 2, P], U8, name="y_scales", align_bytes=64)
            count = len(tiles)
            nc.vector.quantize_mx(
                out=codes[:, :count, :].rearrange("p i q -> p (i q)").bitcast(FP8X4),
                scales=scales[:, :count, :].rearrange("p i q -> p (i q)"),
                in_=kept[("y_grouped", quad)][:, tiles[0] : tiles[0] + count, :, :].rearrange("p i q t -> p (i q t)"),
            )
            kept[("y_codes", n)] = codes
            kept[("y_scales", n)] = scales

        def project(n):
            bank = psum_spare.tile([P, 2, C], F32, name="spare_bank")
            for i in range(len(RESULTS[n][1])):
                nc.tensor.matmul_mx(
                    out=bank[:, i, :],
                    lhsT=kept[("y_codes", n)][:, i, :].bitcast(FP8X4),
                    lhsT_scale=kept[("y_scales", n)][:, i, :],
                    rhs=w_codes[:].bitcast(FP8X4),
                    rhs_scale=w_scales[:],
                    start=True,
                    stop=True,
                )
            kept[("out_bank", n)] = bank

        def store_result(n):
            quad, tiles = RESULTS[n]
            b, h, first_tile = place(QUAD * quad)
            g, t_first = divmod(first_tile + tiles[0], PACK)
            count = len(tiles)
            result = rounds.tile([P, 2, C], F32, name="result", bufs=5)
            nc.scalar.copy(out=result[:, :count, :], in_=kept[("out_bank", n)][:, :count, :])
            tokens_of_pass = out[b, g * K_PASS : (g + 1) * K_PASS, :].rearrange("(p t) c -> p t c", t=PACK)
            nc.sync.dma_start(out=tokens_of_pass[:, t_first : t_first + count, :], in_=result[:, :count, :])

        for unit in range(FLIPS_FIRST):
            transpose_unit(unit)
            copy_unit(unit, nc.vector.tensor_copy if unit == 1 else nc.scalar.copy)

        for r in range(ROUNDS):
            entry_now, r_in_entry = divmod(r, STEPS_PER_ENTRY)
            if r < LOADS:
                load_piece(1, r)
            piece = r_in_entry - STEPS_PER_ENTRY // 2
            if entry_now + 2 < B and 0 <= piece < LOADS:
                load_piece(entry_now + 2, piece)

            for n, unit in enumerate(units_of_round(r - 1)):
                copy_unit(unit, nc.scalar.copy)
            quad = due(r - 1, INVERT_LAG, QUAD, QUADS)
            if quad is not None and quad >= QUADS - BY_TENSOR:
                copy_spread_row_sums(quad)
            attended = attended_in(r - 1)
            for quad, i in attended:
                normalise(quad, i)
            for n in projected_in(r - 1):
                store_result(n)

            flipping = 0 <= r - FLIP_LAG < STEPS
            for piece in range(2 * HALVES):
                if r < STEPS:
                    score_matmul(r, piece // 2, piece % 2)
                if flipping:
                    transpose_probabilities(r - FLIP_LAG, piece)

            if r < STEPS:
                scale_and_bound(r, 0)
            for step in quantised_in(r):
                quantise_probabilities(step)
            for n, (quad, tiles) in enumerate(RESULTS):
                if (quad, tiles[-1]) in attended:
                    quantise_outputs(n)
            quad = due(r, INVERT_LAG, QUAD, QUADS)
            if quad is not None:
                invert_row_sums(quad)
                if quad < QUADS - BY_TENSOR:
                    spread_by_dma(quad)
            if r < STEPS:
                scale_and_bound(r, 1)

            if flipping:
                group_probabilities(r - FLIP_LAG)
            if r < STEPS:
                exponentials(r)

            for unit in units_of_round(r):
                transpose_unit(unit)
            if r == W_ROUND:
                prepare_weights()
            for quad, i in attended_in(r):
                attend(quad, i)
            for n in projected_in(r):
                project(n)
            quad = due(r, INVERT_LAG, QUAD, QUADS)
            if quad is not None and quad >= QUADS - BY_TENSOR:
                spread_by_tensor(quad)

            if r == 0:
                nc.vector.tensor_copy(out=lam1[:], in_=lam1_bf[:])
                nc.vector.tensor_copy(out=lam2[:], in_=lam2_bf[:])
            for b in range(B):
                for chunk in range(CHUNKS):
                    first_round, second_round = mixing_rounds(b, chunk)
                    if r == first_round:
                        scale_values("v1", lam2, b, *divmod(chunk, PASSES))
                    if r == second_round:
                        mix_values(b, *divmod(chunk, PASSES))
            h = r_in_entry - (FIRST_VALUES_LAG if entry_now == 0 else VALUES_LAG)
            if r < STEPS and 0 <= h < H:
                quantise_values(entry_now, h)
